import numpy as np
import ml_dtypes


def mxq(x, axis, fmt="e4m3"):
    dtype, down = {"e4m3": (ml_dtypes.float8_e4m3fn, 7), "e5m2": (ml_dtypes.float8_e5m2, 14)}[fmt]
    v = np.moveaxis(np.asarray(x, np.float32).astype(ml_dtypes.bfloat16).astype(np.float64), axis, -1)
    blocks = v.reshape(v.shape[:-1] + (-1, 32))
    amax = np.abs(blocks).max(-1, keepdims=True)
    byte = np.maximum(np.where(amax > 0, np.frexp(amax)[1] - 1 + 127, 0) - down, 1)
    scale = np.exp2(byte - 127.0)
    codes = (blocks / scale).astype(np.float32).astype(dtype).astype(np.float64)
    return np.moveaxis((codes * scale).reshape(v.shape), -1, axis)


WIDE = False


def mx_kscale(k):
    if not WIDE:
        return np.ones(k)
    levels = np.array([10, -10, 5, -5, 0])
    a = np.random.permutation(np.resize(levels, k // 512 * 4)).reshape(k // 512, 4)
    idx = np.arange(k)
    return np.exp2(a[idx // 512, idx % 128 // 32])


BF16 = ml_dtypes.bfloat16


def bf(x):
    return np.asarray(x, np.float32).astype(BF16)


def f64(x):
    return np.asarray(x).astype(np.float64)


B, N, SR, SI, NH, NV, NC, NLON, NLAT = 2, 96, 1, 128, 4, 4, 32, 8, 8
S = SI * NH
MIN_SIGMA = 1e-10


def setup_inputs():
    s = mx_kscale(S)
    d = np.log2(s.max() / s)
    x0 = np.random.standard_normal((B, N, SR, S, NV, NC)) * 0.2 * np.sqrt(S)
    lon0 = np.random.standard_normal((B, N, SR, SI, NH))
    lat0 = np.random.standard_normal((B, N, SR, SI, NH))
    mus_lon = bf(np.linspace(-1.0, 1.0, NLON) + 0.03 * np.random.standard_normal(NLON))
    mus_lat = bf(np.linspace(-1.0, 1.0, NLAT) + 0.03 * np.random.standard_normal(NLAT))
    sigma = bf(0.4 + 0.2 * np.random.random(1))
    if d.max() > 0:
        sig = float(f64(sigma)[0])
        m0 = float(f64(mus_lon).min())
        lon0 = m0 - np.sqrt((0.3 * sig * lon0) ** 2 + 2.0 * np.log(2.0) * sig ** 2 * d.reshape(SI, NH))
    return {"x": bf(x0 * (2.0 ** d)[:, None, None]),
            "coords_lon": bf(lon0),
            "coords_lat": bf(lat0),
            "mus_lon": mus_lon,
            "mus_lat": mus_lat,
            "sigma": sigma}


def reference(x, coords_lon, coords_lat, mus_lon, mus_lat, sigma):
    x, coords_lon, coords_lat = f64(x), f64(coords_lon), f64(coords_lat)
    mus_lon, mus_lat, sigma = f64(mus_lon), f64(mus_lat), f64(sigma)
    b, n, sr, si, nh = coords_lon.shape
    nv, nc = x.shape[-2:]
    nlon, nlat = mus_lon.shape[0], mus_lat.shape[0]
    sig = np.maximum(sigma, MIN_SIGMA)
    wlon = np.exp(-0.5 * ((coords_lon[..., None] - mus_lon) / sig) ** 2)
    wlat = np.exp(-0.5 * ((coords_lat[..., None] - mus_lat) / sig) ** 2)
    w = (wlon[..., :, None] * wlat[..., None, :]).reshape(b, n, sr, si * nh, nlon, nlat)
    w = w / np.sum(w, axis=3, keepdims=True)
    wq = mxq(w, 3, "e4m3").reshape(b, n, sr, si * nh, nlon * nlat)
    xq = mxq(x, 3, "e4m3").reshape(b, n, sr, si * nh, nv * nc)
    out = xq.transpose(0, 1, 2, 4, 3) @ wq
    out = out.reshape(b, n, sr, nv, nc, nlon, nlat).transpose(0, 1, 2, 3, 5, 6, 4)
    return out.reshape(b, n * sr, nv, nlon, nlat, nc)

@@ -1,0 +1,253 @@
+import concourse.mybir as mybir
+from concourse.masks import make_identity
+
+F32 = mybir.dt.float32
+BF16 = mybir.dt.bfloat16
+U32 = mybir.dt.uint32
+U8 = mybir.dt.uint8
+I32 = mybir.dt.int32
+FP8X4 = mybir.dt.float8_e4m3fn_x4
+ACT = mybir.ActivationFunctionType
+ALU = mybir.AluOpType
+
+P = 128
+PACK = 4
+BATCH = 2
+NWIN = 96
+OFFS = 8
+COLS_W = OFFS * OFFS
+COLS_X = 128
+CHAN = 32
+MIN_SIGMA = 1e-10
+
+PAIRS = 4
+CHUNKS = NWIN // PAIRS
+BLOCK = 2
+AHEAD = 2
+W_SETS = 3
+
+FLOPS = 2 * BATCH * NWIN * P * PACK * COLS_X * COLS_W
+
+
+def tile_normal_nolayer_kernel(tc, x, coords_lon, coords_lat, mus_lon, mus_lat, sigma, out):
+    nc = tc.nc
+
+    x_view = x.rearrange("b n o (k t) v c -> b k (n o) (t v c)", t=PACK)
+    out_view = out.rearrange("b n v p q c -> b (p q) (n v) c")
+    coord_rows = [
+        coords_lon.rearrange("b n o i h -> (b n o) (i h)"),
+        coords_lat.rearrange("b n o i h -> (b n o) (i h)"),
+    ]
+
+    with tc.tile_pool(name="keep", bufs=1) as keep, tc.tile_pool(name="head", bufs=1) as head, tc.tile_pool(
+        name="xin", bufs=AHEAD + 1
+    ) as xin, tc.tile_pool(name="work", bufs=3) as work, tc.psum_pool(name="psum", bufs=2) as psum:
+        ident_bf = keep.tile([P, P], BF16)
+        make_identity(nc, ident_bf[:])
+        ident_f = keep.tile([P, P], F32)
+        make_identity(nc, ident_f[:])
+        ones = keep.tile([P, 1], F32)
+        nc.vector.memset(ones[:], 1.0)
+
+        sig_bf = keep.tile([P, 1], BF16)
+        nc.sync.dma_start(out=sig_bf[:], in_=sigma.partition_broadcast(P))
+        mu_lon = keep.tile([P, OFFS], BF16)
+        nc.sync.dma_start(out=mu_lon[:], in_=mus_lon.partition_broadcast(P))
+        mu_lat = keep.tile([P, OFFS], BF16)
+        nc.sync.dma_start(out=mu_lat[:], in_=mus_lat.partition_broadcast(P))
+        mu_tiles = [mu_lon, mu_lat]
+
+        sig_f = keep.tile([P, 1], F32)
+        nc.vector.tensor_scalar_max(out=sig_f[:], in0=sig_bf[:], scalar1=MIN_SIGMA)
+        inv_sig = keep.tile([P, 1], F32)
+        nc.vector.reciprocal(out=inv_sig[:], in_=sig_f[:])
+
+        w_codes = []
+        w_scales = []
+        for i in range(W_SETS):
+            codes = keep.tile([P, PAIRS, 4 * COLS_W], U32, name="w_codes%d" % i, align_bytes=64)
+            nc.vector.memset(codes[:].bitcast(I32), 0)
+            w_codes.append(codes)
+            scales = keep.tile([P, PAIRS, 4 * COLS_W], U8, name="w_scales%d" % i, align_bytes=64)
+            nc.vector.memset(scales[:].bitcast(I32), 0)
+            w_scales.append(scales)
+
+        coord = keep.tile([P, 2, NWIN, PACK, BATCH], BF16)
+        for a in range(2):
+            for b in range(BATCH):
+                first_row = b * (BATCH * NWIN - P)
+                first_col = b * (P - NWIN)
+                rows = head.tile([P, P * PACK], BF16, name="rows%d%d" % (a, b))
+                nc.sync.dma_start(out=rows[:], in_=coord_rows[a][first_row : first_row + P, :])
+                sorted_rows = head.tile([P, PACK, P], BF16, name="sorted%d%d" % (a, b))
+                nc.vector.tensor_copy(out=sorted_rows[:], in_=rows[:].rearrange("w (i t) -> w t i", t=PACK))
+                turned = psum.tile([P, PACK, P], BF16, tag="spread")
+                for t in range(PACK):
+                    nc.tensor.transpose(turned[:, t, :], sorted_rows[:, t, :], ident_bf[:])
+                nc.vector.tensor_copy(
+                    out=coord[:, a, :, :, b],
+                    in_=turned[:, :, first_col : first_col + NWIN].rearrange("k t n -> k n t"),
+                )
+
+        coord_flat = coord[:].rearrange("k a n t b -> k a (n t b)")
+        entries = PAIRS * PACK * BATCH
+
+        gauss_tiles = {}
+
+        def distances(i):
+            span = slice(i * entries, (i + 1) * entries)
+            gauss = work.tile([P, 2, entries, OFFS], F32, bufs=5)
+            for a in range(2):
+                nc.gpsimd.tensor_tensor(
+                    out=gauss[:, a],
+                    in0=coord_flat[:, a, span].unsqueeze(2).to_broadcast([P, entries, OFFS]),
+                    in1=mu_tiles[a][:].unsqueeze(1).to_broadcast([P, entries, OFFS]),
+                    op=ALU.subtract,
+                )
+            gauss_tiles[i] = gauss
+
+        def gaussians(i):
+            gauss = gauss_tiles[i]
+            nc.scalar.activation(out=gauss[:], in_=gauss[:], func=ACT.Square, scale=inv_sig[:])
+            nc.scalar.activation(out=gauss[:], in_=gauss[:], func=ACT.Exp, scale=-0.5)
+
+        raw_tiles = {}
+        grouped_tiles = {}
+        x_code_tiles = {}
+        x_scale_tiles = {}
+        product_tiles = {}
+        sum_tiles = {}
+        spread_tiles = {}
+        acc_tiles = {}
+        result_tiles = {}
+
+        def load_x(block):
+            raw = xin.tile([P, BATCH, BLOCK * PAIRS, PACK * COLS_X], BF16)
+            pairs = slice(block * BLOCK * PAIRS, (block + 1) * BLOCK * PAIRS)
+            for b in range(BATCH):
+                nc.sync.dma_start(out=raw[:, b], in_=x_view[b, :, pairs, :])
+            raw_tiles[block] = raw
+
+        def regroup_x(i):
+            grouped = work.tile([P, BATCH, PAIRS, COLS_X, PACK], BF16, align_bytes=64, bufs=4)
+            pairs = slice((i % BLOCK) * PAIRS, (i % BLOCK + 1) * PAIRS)
+            for b in range(BATCH):
+                nc.scalar.copy(
+                    out=grouped[:, b],
+                    in_=raw_tiles[i // BLOCK][:, b, pairs, :].rearrange("k j (t c) -> k j c t", t=PACK),
+                )
+            grouped_tiles[i] = grouped
+
+        def quantise_x(i):
+            x_codes = work.tile([P, BATCH, PAIRS, COLS_X], U32, align_bytes=64)
+            x_scales = work.tile([P, BATCH, PAIRS, COLS_X], U8, align_bytes=64)
+            nc.vector.quantize_mx(
+                out=x_codes[:].rearrange("k b j c -> k (b j c)").bitcast(FP8X4),
+                scales=x_scales[:].rearrange("k b j c -> k (b j c)"),
+                in_=grouped_tiles.pop(i)[:].rearrange("k b j c t -> k (b j c t)"),
+            )
+            x_code_tiles[i] = x_codes
+            x_scale_tiles[i] = x_scales
+
+        def products(i):
+            gauss = gauss_tiles.pop(i)
+            g = work.tile([P, PAIRS, PACK, BATCH * COLS_W], F32)
+            nc.vector.tensor_tensor(
+                out=g[:].rearrange("k j t (b p q) -> k (j t b) p q", b=BATCH, p=OFFS),
+                in0=gauss[:, 0].unsqueeze(3).to_broadcast([P, entries, OFFS, OFFS]),
+                in1=gauss[:, 1].unsqueeze(2).to_broadcast([P, entries, OFFS, OFFS]),
+                op=ALU.mult,
+            )
+            sums = psum.tile([P, PAIRS], F32, tag="sums")
+            for j in range(PAIRS):
+                for t in range(PACK):
+                    nc.tensor.matmul(
+                        out=sums[:, j : j + 1], lhsT=g[:, j, t, :], rhs=ones[:], start=(t == 0), stop=(t == PACK - 1)
+                    )
+            product_tiles[i] = g
+            sum_tiles[i] = sums
+
+        def normalisers(i):
+            inverse = work.tile([P, PAIRS], F32)
+            nc.vector.reciprocal(out=inverse[:], in_=sum_tiles.pop(i)[:])
+            spread = psum.tile([P, PAIRS, BATCH * COLS_W], F32, tag="spread")
+            for j in range(PAIRS):
+                nc.tensor.transpose(spread[:, j, :], inverse[:, j : j + 1].to_broadcast([P, P]), ident_f[:])
+            spread_tiles[i] = spread
+
+        def weights(i):
+            width = BATCH * COLS_W
+            w_bf = work.tile([P, PAIRS, width, PACK], BF16, align_bytes=64)
+            nc.vector.tensor_tensor(
+                out=w_bf[:],
+                in0=product_tiles.pop(i)[:].rearrange("k j t m -> k j m t"),
+                in1=spread_tiles.pop(i)[:].unsqueeze(3).to_broadcast([P, PAIRS, width, PACK]),
+                op=ALU.mult,
+            )
+            codes = w_codes[i % W_SETS]
+            scales = w_scales[i % W_SETS]
+            for j in range(PAIRS):
+                for b in range(BATCH):
+                    place = slice(b * 3 * COLS_W, b * 3 * COLS_W + COLS_W)
+                    nc.vector.quantize_mx(
+                        out=codes[:, j, place].bitcast(FP8X4),
+                        scales=scales[:, j, place],
+                        in_=w_bf[:, j, b * COLS_W : (b + 1) * COLS_W, :].rearrange("k m t -> k (m t)"),
+                    )
+
+        def contract(i):
+            codes = w_codes[i % W_SETS]
+            scales = w_scales[i % W_SETS]
+            x_codes = x_code_tiles.pop(i)
+            x_scales = x_scale_tiles.pop(i)
+            acc = psum.tile([P, PAIRS, COLS_X], F32, tag="acc")
+            for j in range(PAIRS):
+                for b in range(BATCH):
+                    half = slice(b * 2 * COLS_W, (b + 1) * 2 * COLS_W)
+                    nc.tensor.matmul_mx(
+                        out=acc[:, j, :],
+                        lhsT=codes[:, j, half].bitcast(FP8X4),
+                        lhsT_scale=scales[:, j, half],
+                        rhs=x_codes[:, b, j, :].bitcast(FP8X4),
+                        rhs_scale=x_scales[:, b, j, :],
+                        start=(b == 0),
+                        stop=(b == BATCH - 1),
+                    )
+            acc_tiles[i] = acc
+
+        def store(i):
+            block = i // BLOCK
+            if i % BLOCK == 0:
+                result = work.tile([P, BLOCK, PAIRS, COLS_X], F32)
+                result_tiles[block] = result
+            result = result_tiles[block]
+            nc.scalar.copy(out=result[:, i % BLOCK], in_=acc_tiles.pop(i)[:])
+            if i % BLOCK == BLOCK - 1:
+                rows_nv = BLOCK * PAIRS * (COLS_X // CHAN)
+                for b in range(BATCH):
+                    nc.sync.dma_start(
+                        out=out_view[b, :, block * rows_nv : (block + 1) * rows_nv, :],
+                        in_=result[b * COLS_W : (b + 1) * COLS_W].rearrange("m u j (v c) -> m (u j v) c", c=CHAN),
+                    )
+
+        with tc.manual_schedule():
+            for step in range(-1 - AHEAD * BLOCK, CHUNKS + 4):
+                ask = step + 1 + AHEAD * BLOCK
+                if 0 <= ask < CHUNKS and ask % BLOCK == 0:
+                    load_x(ask // BLOCK)
+                if 0 <= step + 3 < CHUNKS:
+                    distances(step + 3)
+                if 0 <= step + 2 < CHUNKS:
+                    gaussians(step + 2)
+                if 0 <= step + 1 < CHUNKS:
+                    regroup_x(step + 1)
+                if 0 <= step < CHUNKS:
+                    products(step)
+                if 0 <= step - 1 < CHUNKS:
+                    normalisers(step - 1)
+                    quantise_x(step - 1)
+                if 0 <= step - 2 < CHUNKS:
+                    weights(step - 2)
+                    contract(step - 2)
+                if 0 <= step - 3 < CHUNKS:
+                    store(step - 3)

@@ -46,8 +46,6 @@ def tile_normal_nolayer_kernel(tc, x, coords_lon, coords_lat, mus_lon, mus_lat, 
         make_identity(nc, ident_bf[:])
         ident_f = keep.tile([P, P], F32)
         make_identity(nc, ident_f[:])
-        ones = keep.tile([P, 1], F32)
-        nc.vector.memset(ones[:], 1.0)
 
         sig_bf = keep.tile([P, 1], BF16)
         nc.sync.dma_start(out=sig_bf[:], in_=sigma.partition_broadcast(P))
@@ -158,18 +156,25 @@ def tile_normal_nolayer_kernel(tc, x, coords_lon, coords_lat, mus_lon, mus_lat, 
                 in1=gauss[:, 1].unsqueeze(2).to_broadcast([P, entries, OFFS, OFFS]),
                 op=ALU.mult,
             )
-            sums = psum.tile([P, PAIRS], F32, tag="sums")
+            sums = psum.tile([P, PAIRS, P], F32, tag="sums")
             for j in range(PAIRS):
                 for t in range(PACK):
                     nc.tensor.matmul(
-                        out=sums[:, j : j + 1], lhsT=g[:, j, t, :], rhs=ones[:], start=(t == 0), stop=(t == PACK - 1)
+                        out=sums[:, j, :],
+                        lhsT=g[:, j, t, :],
+                        rhs=ident_f[:],
+                        is_transpose=True,
+                        start=(t == 0),
+                        stop=(t == PACK - 1),
                     )
             product_tiles[i] = g
             sum_tiles[i] = sums
 
         def normalisers(i):
+            total = work.tile([P, PAIRS], F32)
+            nc.vector.tensor_reduce(out=total[:], in_=sum_tiles.pop(i)[:], axis=mybir.AxisListType.X, op=ALU.add)
             inverse = work.tile([P, PAIRS], F32)
-            nc.vector.reciprocal(out=inverse[:], in_=sum_tiles.pop(i)[:])
+            nc.vector.reciprocal(out=inverse[:], in_=total[:])
             spread = psum.tile([P, PAIRS, BATCH * COLS_W], F32, tag="spread")
             for j in range(PAIRS):
                 nc.tensor.transpose(spread[:, j, :], inverse[:, j : j + 1].to_broadcast([P, P]), ident_f[:])

@@ -96,7 +96,7 @@ def tile_normal_nolayer_kernel(tc, x, coords_lon, coords_lat, mus_lon, mus_lat, 
             span = slice(i * entries, (i + 1) * entries)
             gauss = work.tile([P, 2, entries, OFFS], F32, bufs=5)
             for a in range(2):
-                nc.gpsimd.tensor_tensor(
+                nc.vector.tensor_tensor(
                     out=gauss[:, a],
                     in0=coord_flat[:, a, span].unsqueeze(2).to_broadcast([P, entries, OFFS]),
                     in1=mu_tiles[a][:].unsqueeze(1).to_broadcast([P, entries, OFFS]),

@@ -25,6 +25,7 @@ CHUNKS = NWIN // PAIRS
 BLOCK = 2
 AHEAD = 2
 W_SETS = 3
+RUN = 4
 
 FLOPS = 2 * BATCH * NWIN * P * PACK * COLS_X * COLS_W
 
@@ -96,7 +97,7 @@ def tile_normal_nolayer_kernel(tc, x, coords_lon, coords_lat, mus_lon, mus_lat, 
             span = slice(i * entries, (i + 1) * entries)
             gauss = work.tile([P, 2, entries, OFFS], F32, bufs=5)
             for a in range(2):
-                nc.vector.tensor_tensor(
+                nc.gpsimd.tensor_tensor(
                     out=gauss[:, a],
                     in0=coord_flat[:, a, span].unsqueeze(2).to_broadcast([P, entries, OFFS]),
                     in1=mu_tiles[a][:].unsqueeze(1).to_broadcast([P, entries, OFFS]),
@@ -117,6 +118,8 @@ def tile_normal_nolayer_kernel(tc, x, coords_lon, coords_lat, mus_lon, mus_lat, 
         sum_tiles = {}
         spread_tiles = {}
         acc_tiles = {}
+        total_tiles = {}
+        w_tiles = {}
         result_tiles = {}
 
         def load_x(block):
@@ -128,12 +131,14 @@ def tile_normal_nolayer_kernel(tc, x, coords_lon, coords_lat, mus_lon, mus_lat, 
 
         def regroup_x(i):
             grouped = work.tile([P, BATCH, PAIRS, COLS_X, PACK], BF16, align_bytes=64, bufs=4)
-            pairs = slice((i % BLOCK) * PAIRS, (i % BLOCK + 1) * PAIRS)
+            first = (i % BLOCK) * PAIRS
+            raw = raw_tiles[i // BLOCK]
             for b in range(BATCH):
-                nc.scalar.copy(
-                    out=grouped[:, b],
-                    in_=raw_tiles[i // BLOCK][:, b, pairs, :].rearrange("k j (t c) -> k j c t", t=PACK),
-                )
+                for j in range(PAIRS):
+                    nc.scalar.copy(
+                        out=grouped[:, b, j].rearrange("k (c r) t -> k c t r", r=RUN),
+                        in_=raw[:, b, first + j, :].rearrange("k (t c r) -> k c t r", t=PACK, r=RUN),
+                    )
             grouped_tiles[i] = grouped
 
         def quantise_x(i):
@@ -170,11 +175,14 @@ def tile_normal_nolayer_kernel(tc, x, coords_lon, coords_lat, mus_lon, mus_lat, 
             product_tiles[i] = g
             sum_tiles[i] = sums
 
-        def normalisers(i):
+        def totals(i):
             total = work.tile([P, PAIRS], F32)
             nc.vector.tensor_reduce(out=total[:], in_=sum_tiles.pop(i)[:], axis=mybir.AxisListType.X, op=ALU.add)
+            total_tiles[i] = total
+
+        def normalisers(i):
             inverse = work.tile([P, PAIRS], F32)
-            nc.vector.reciprocal(out=inverse[:], in_=total[:])
+            nc.vector.reciprocal(out=inverse[:], in_=total_tiles.pop(i)[:])
             spread = psum.tile([P, PAIRS, BATCH * COLS_W], F32, tag="spread")
             for j in range(PAIRS):
                 nc.tensor.transpose(spread[:, j, :], inverse[:, j : j + 1].to_broadcast([P, P]), ident_f[:])
@@ -189,6 +197,10 @@ def tile_normal_nolayer_kernel(tc, x, coords_lon, coords_lat, mus_lon, mus_lat, 
                 in1=spread_tiles.pop(i)[:].unsqueeze(3).to_broadcast([P, PAIRS, width, PACK]),
                 op=ALU.mult,
             )
+            w_tiles[i] = w_bf
+
+        def quantise_w(i):
+            w_bf = w_tiles.pop(i)
             codes = w_codes[i % W_SETS]
             scales = w_scales[i % W_SETS]
             for j in range(PAIRS):
@@ -246,13 +258,18 @@ def tile_normal_nolayer_kernel(tc, x, coords_lon, coords_lat, mus_lon, mus_lat, 
                     gaussians(step + 2)
                 if 0 <= step + 1 < CHUNKS:
                     regroup_x(step + 1)
+                if 0 <= step - 1 < CHUNKS:
+                    totals(step - 1)
                 if 0 <= step < CHUNKS:
                     products(step)
                 if 0 <= step - 1 < CHUNKS:
                     normalisers(step - 1)
-                    quantise_x(step - 1)
                 if 0 <= step - 2 < CHUNKS:
                     weights(step - 2)
+                if 0 <= step - 1 < CHUNKS:
+                    quantise_x(step - 1)
+                if 0 <= step - 2 < CHUNKS:
+                    quantise_w(step - 2)
                     contract(step - 2)
                 if 0 <= step - 3 < CHUNKS:
                     store(step - 3)

@@ -26,6 +26,7 @@ BLOCK = 2
 AHEAD = 2
 W_SETS = 3
 RUN = 4
+GP_PAIRS = 2
 
 FLOPS = 2 * BATCH * NWIN * P * PACK * COLS_X * COLS_W
 
@@ -152,15 +153,24 @@ def tile_normal_nolayer_kernel(tc, x, coords_lon, coords_lat, mus_lon, mus_lat, 
             x_code_tiles[i] = x_codes
             x_scale_tiles[i] = x_scales
 
-        def products(i):
-            gauss = gauss_tiles.pop(i)
-            g = work.tile([P, PAIRS, PACK, BATCH * COLS_W], F32)
-            nc.vector.tensor_tensor(
-                out=g[:].rearrange("k j t (b p q) -> k (j t b) p q", b=BATCH, p=OFFS),
-                in0=gauss[:, 0].unsqueeze(3).to_broadcast([P, entries, OFFS, OFFS]),
-                in1=gauss[:, 1].unsqueeze(2).to_broadcast([P, entries, OFFS, OFFS]),
+        def outer_products(engine, g, gauss, first, last):
+            span = slice(first * PACK * BATCH, last * PACK * BATCH)
+            count = (last - first) * PACK * BATCH
+            engine.tensor_tensor(
+                out=g[:, first:last].rearrange("k j t (b p q) -> k (j t b) p q", b=BATCH, p=OFFS),
+                in0=gauss[:, 0, span, :].unsqueeze(3).to_broadcast([P, count, OFFS, OFFS]),
+                in1=gauss[:, 1, span, :].unsqueeze(2).to_broadcast([P, count, OFFS, OFFS]),
                 op=ALU.mult,
             )
+
+        def products_on_gpsimd(i):
+            g = work.tile([P, PAIRS, PACK, BATCH * COLS_W], F32, bufs=5)
+            outer_products(nc.gpsimd, g, gauss_tiles[i], PAIRS - GP_PAIRS, PAIRS)
+            product_tiles[i] = g
+
+        def products(i):
+            g = product_tiles[i]
+            outer_products(nc.vector, g, gauss_tiles.pop(i), 0, PAIRS - GP_PAIRS)
             sums = psum.tile([P, PAIRS, P], F32, tag="sums")
             for j in range(PAIRS):
                 for t in range(PACK):
@@ -172,7 +182,6 @@ def tile_normal_nolayer_kernel(tc, x, coords_lon, coords_lat, mus_lon, mus_lat, 
                         start=(t == 0),
                         stop=(t == PACK - 1),
                     )
-            product_tiles[i] = g
             sum_tiles[i] = sums
 
         def totals(i):
@@ -257,6 +266,7 @@ def tile_normal_nolayer_kernel(tc, x, coords_lon, coords_lat, mus_lon, mus_lat, 
                 if 0 <= step + 2 < CHUNKS:
                     gaussians(step + 2)
                 if 0 <= step + 1 < CHUNKS:
+                    products_on_gpsimd(step + 1)
                     regroup_x(step + 1)
                 if 0 <= step - 1 < CHUNKS:
                     totals(step - 1)

@@ -50,12 +50,16 @@ def tile_normal_nolayer_kernel(tc, x, coords_lon, coords_lat, mus_lon, mus_lat, 
         make_identity(nc, ident_f[:])
 
         sig_bf = keep.tile([P, 1], BF16)
-        nc.sync.dma_start(out=sig_bf[:], in_=sigma.partition_broadcast(P))
+        nc.scalar.dma_start(out=sig_bf[:], in_=sigma.partition_broadcast(P))
         mu_lon = keep.tile([P, OFFS], BF16)
-        nc.sync.dma_start(out=mu_lon[:], in_=mus_lon.partition_broadcast(P))
+        nc.scalar.dma_start(out=mu_lon[:], in_=mus_lon.partition_broadcast(P))
         mu_lat = keep.tile([P, OFFS], BF16)
-        nc.sync.dma_start(out=mu_lat[:], in_=mus_lat.partition_broadcast(P))
+        nc.scalar.dma_start(out=mu_lat[:], in_=mus_lat.partition_broadcast(P))
         mu_tiles = [mu_lon, mu_lat]
+
+        warm = keep.tile([P, 1], F32)
+        nc.vector.memset(warm[:], 0.0)
+        nc.scalar.activation(out=warm[:], in_=warm[:], func=ACT.Exp)
 
         sig_f = keep.tile([P, 1], F32)
         nc.vector.tensor_scalar_max(out=sig_f[:], in0=sig_bf[:], scalar1=MIN_SIGMA)
@@ -106,9 +110,12 @@ def tile_normal_nolayer_kernel(tc, x, coords_lon, coords_lat, mus_lon, mus_lat, 
                 )
             gauss_tiles[i] = gauss
 
-        def gaussians(i):
+        def squares(i):
             gauss = gauss_tiles[i]
             nc.scalar.activation(out=gauss[:], in_=gauss[:], func=ACT.Square, scale=inv_sig[:])
+
+        def gaussians(i):
+            gauss = gauss_tiles[i]
             nc.scalar.activation(out=gauss[:], in_=gauss[:], func=ACT.Exp, scale=-0.5)
 
         raw_tiles = {}
@@ -135,11 +142,10 @@ def tile_normal_nolayer_kernel(tc, x, coords_lon, coords_lat, mus_lon, mus_lat, 
             first = (i % BLOCK) * PAIRS
             raw = raw_tiles[i // BLOCK]
             for b in range(BATCH):
-                for j in range(PAIRS):
-                    nc.scalar.copy(
-                        out=grouped[:, b, j].rearrange("k (c r) t -> k c t r", r=RUN),
-                        in_=raw[:, b, first + j, :].rearrange("k (t c r) -> k c t r", t=PACK, r=RUN),
-                    )
+                nc.scalar.copy(
+                    out=grouped[:, b].rearrange("k j (c r) t -> k j c t r", r=RUN),
+                    in_=raw[:, b, first : first + PAIRS, :].rearrange("k j (t c r) -> k j c t r", t=PACK, r=RUN),
+                )
             grouped_tiles[i] = grouped
 
         def quantise_x(i):
@@ -212,14 +218,13 @@ def tile_normal_nolayer_kernel(tc, x, coords_lon, coords_lat, mus_lon, mus_lat, 
             w_bf = w_tiles.pop(i)
             codes = w_codes[i % W_SETS]
             scales = w_scales[i % W_SETS]
+            inner = slice(COLS_W, 3 * COLS_W)
             for j in range(PAIRS):
-                for b in range(BATCH):
-                    place = slice(b * 3 * COLS_W, b * 3 * COLS_W + COLS_W)
-                    nc.vector.quantize_mx(
-                        out=codes[:, j, place].bitcast(FP8X4),
-                        scales=scales[:, j, place],
-                        in_=w_bf[:, j, b * COLS_W : (b + 1) * COLS_W, :].rearrange("k m t -> k (m t)"),
-                    )
+                nc.vector.quantize_mx(
+                    out=codes[:, j, inner].bitcast(FP8X4),
+                    scales=scales[:, j, inner],
+                    in_=w_bf[:, j].rearrange("k m t -> k (m t)"),
+                )
 
         def contract(i):
             codes = w_codes[i % W_SETS]
@@ -251,9 +256,10 @@ def tile_normal_nolayer_kernel(tc, x, coords_lon, coords_lat, mus_lon, mus_lat, 
             if i % BLOCK == BLOCK - 1:
                 rows_nv = BLOCK * PAIRS * (COLS_X // CHAN)
                 for b in range(BATCH):
+                    lanes = slice((1 - b) * COLS_W, (2 - b) * COLS_W)
                     nc.sync.dma_start(
                         out=out_view[b, :, block * rows_nv : (block + 1) * rows_nv, :],
-                        in_=result[b * COLS_W : (b + 1) * COLS_W].rearrange("m u j (v c) -> m (u j v) c", c=CHAN),
+                        in_=result[lanes].rearrange("m u j (v c) -> m (u j v) c", c=CHAN),
                     )
 
         with tc.manual_schedule():
@@ -264,10 +270,12 @@ def tile_normal_nolayer_kernel(tc, x, coords_lon, coords_lat, mus_lon, mus_lat, 
                 if 0 <= step + 3 < CHUNKS:
                     distances(step + 3)
                 if 0 <= step + 2 < CHUNKS:
-                    gaussians(step + 2)
+                    squares(step + 2)
                 if 0 <= step + 1 < CHUNKS:
                     products_on_gpsimd(step + 1)
                     regroup_x(step + 1)
+                if 0 <= step + 2 < CHUNKS:
+                    gaussians(step + 2)
                 if 0 <= step - 1 < CHUNKS:
                     totals(step - 1)
                 if 0 <= step < CHUNKS:

@@ -26,7 +26,7 @@ BLOCK = 2
 AHEAD = 2
 W_SETS = 3
 RUN = 4
-GP_PAIRS = 2
+GP_PAIRS = 3
 
 FLOPS = 2 * BATCH * NWIN * P * PACK * COLS_X * COLS_W
 

@@ -27,6 +27,7 @@ AHEAD = 2
 W_SETS = 3
 RUN = 4
 GP_PAIRS = 3
+SQ_CHUNKS = 4
 
 FLOPS = 2 * BATCH * NWIN * P * PACK * COLS_X * COLS_W
 
@@ -65,6 +66,13 @@ def tile_normal_nolayer_kernel(tc, x, coords_lon, coords_lat, mus_lon, mus_lat, 
         nc.vector.tensor_scalar_max(out=sig_f[:], in0=sig_bf[:], scalar1=MIN_SIGMA)
         inv_sig = keep.tile([P, 1], F32)
         nc.vector.reciprocal(out=inv_sig[:], in_=sig_f[:])
+        neg_mu = []
+        for a in range(2):
+            shifted = keep.tile([P, OFFS], F32, name="neg_mu%d" % a)
+            nc.vector.tensor_scalar(
+                out=shifted[:], in0=mu_tiles[a][:], scalar1=inv_sig[:], scalar2=-1.0, op0=ALU.mult, op1=ALU.mult
+            )
+            neg_mu.append(shifted)
 
         w_codes = []
         w_scales = []
@@ -76,7 +84,7 @@ def tile_normal_nolayer_kernel(tc, x, coords_lon, coords_lat, mus_lon, mus_lat, 
             nc.vector.memset(scales[:].bitcast(I32), 0)
             w_scales.append(scales)
 
-        coord = keep.tile([P, 2, NWIN, PACK, BATCH], BF16)
+        coord = keep.tile([P, 2, NWIN, BATCH, PACK], BF16)
         for a in range(2):
             for b in range(BATCH):
                 first_row = b * (BATCH * NWIN - P)
@@ -89,34 +97,38 @@ def tile_normal_nolayer_kernel(tc, x, coords_lon, coords_lat, mus_lon, mus_lat, 
                 for t in range(PACK):
                     nc.tensor.transpose(turned[:, t, :], sorted_rows[:, t, :], ident_bf[:])
                 nc.vector.tensor_copy(
-                    out=coord[:, a, :, :, b],
+                    out=coord[:, a, :, b, :],
                     in_=turned[:, :, first_col : first_col + NWIN].rearrange("k t n -> k n t"),
                 )
 
-        coord_flat = coord[:].rearrange("k a n t b -> k a (n t b)")
-        entries = PAIRS * PACK * BATCH
+        windows = PAIRS * BATCH
 
         gauss_tiles = {}
 
-        def distances(i):
-            span = slice(i * entries, (i + 1) * entries)
-            gauss = work.tile([P, 2, entries, OFFS], F32, bufs=5)
-            for a in range(2):
-                nc.gpsimd.tensor_tensor(
-                    out=gauss[:, a],
-                    in0=coord_flat[:, a, span].unsqueeze(2).to_broadcast([P, entries, OFFS]),
-                    in1=mu_tiles[a][:].unsqueeze(1).to_broadcast([P, entries, OFFS]),
-                    op=ALU.subtract,
+        def squares(group, part):
+            if part == 0:
+                new_tile = work.tile([P, 2, SQ_CHUNKS * windows, OFFS, PACK], F32, name="gauss", bufs=3)
+                gauss_tiles[group] = new_tile
+            gauss = gauss_tiles[group]
+            pairs = slice(group * SQ_CHUNKS * PAIRS, (group + 1) * SQ_CHUNKS * PAIRS)
+            share = 2 * OFFS // SQ_CHUNKS
+            for number in range(part * share, (part + 1) * share):
+                a, o = divmod(number, OFFS)
+                nc.scalar.activation(
+                    out=gauss[:, a, :, o, :],
+                    in_=coord[:, a, pairs].rearrange("k n b t -> k (n b) t"),
+                    func=ACT.Square,
+                    scale=inv_sig[:],
+                    bias=neg_mu[a][:, o : o + 1],
                 )
-            gauss_tiles[i] = gauss
 
-        def squares(i):
-            gauss = gauss_tiles[i]
-            nc.scalar.activation(out=gauss[:], in_=gauss[:], func=ACT.Square, scale=inv_sig[:])
+        def chunk_windows(i, first, last):
+            start = (i % SQ_CHUNKS) * windows
+            return slice(start + first * BATCH, start + last * BATCH)
 
         def gaussians(i):
-            gauss = gauss_tiles[i]
-            nc.scalar.activation(out=gauss[:], in_=gauss[:], func=ACT.Exp, scale=-0.5)
+            part = gauss_tiles[i // SQ_CHUNKS][:, :, chunk_windows(i, 0, PAIRS)]
+            nc.scalar.activation(out=part, in_=part, func=ACT.Exp, scale=-0.5)
 
         raw_tiles = {}
         grouped_tiles = {}
@@ -159,30 +171,33 @@ def tile_normal_nolayer_kernel(tc, x, coords_lon, coords_lat, mus_lon, mus_lat, 
             x_code_tiles[i] = x_codes
             x_scale_tiles[i] = x_scales
 
-        def outer_products(engine, g, gauss, first, last):
-            span = slice(first * PACK * BATCH, last * PACK * BATCH)
-            count = (last - first) * PACK * BATCH
+        def outer_products(engine, g, i, first, last):
+            gauss = gauss_tiles[i // SQ_CHUNKS]
+            span = chunk_windows(i, first, last)
+            count = (last - first) * BATCH
             engine.tensor_tensor(
-                out=g[:, first:last].rearrange("k j t (b p q) -> k (j t b) p q", b=BATCH, p=OFFS),
-                in0=gauss[:, 0, span, :].unsqueeze(3).to_broadcast([P, count, OFFS, OFFS]),
-                in1=gauss[:, 1, span, :].unsqueeze(2).to_broadcast([P, count, OFFS, OFFS]),
+                out=g[:, first:last].rearrange("k j (b p q) t -> k (j b) p q t", b=BATCH, p=OFFS),
+                in0=gauss[:, 0, span].unsqueeze(3).to_broadcast([P, count, OFFS, OFFS, PACK]),
+                in1=gauss[:, 1, span].unsqueeze(2).to_broadcast([P, count, OFFS, OFFS, PACK]),
                 op=ALU.mult,
             )
 
         def products_on_gpsimd(i):
-            g = work.tile([P, PAIRS, PACK, BATCH * COLS_W], F32, bufs=5)
-            outer_products(nc.gpsimd, g, gauss_tiles[i], PAIRS - GP_PAIRS, PAIRS)
+            g = work.tile([P, PAIRS, BATCH * COLS_W, PACK], F32, bufs=5)
+            outer_products(nc.gpsimd, g, i, PAIRS - GP_PAIRS, PAIRS)
             product_tiles[i] = g
 
         def products(i):
             g = product_tiles[i]
-            outer_products(nc.vector, g, gauss_tiles.pop(i), 0, PAIRS - GP_PAIRS)
+            outer_products(nc.vector, g, i, 0, PAIRS - GP_PAIRS)
+            if i % SQ_CHUNKS == SQ_CHUNKS - 1:
+                gauss_tiles.pop(i // SQ_CHUNKS)
             sums = psum.tile([P, PAIRS, P], F32, tag="sums")
             for j in range(PAIRS):
                 for t in range(PACK):
                     nc.tensor.matmul(
                         out=sums[:, j, :],
-                        lhsT=g[:, j, t, :],
+                        lhsT=g[:, j, :, t],
                         rhs=ident_f[:],
                         is_transpose=True,
                         start=(t == 0),
@@ -208,7 +223,7 @@ def tile_normal_nolayer_kernel(tc, x, coords_lon, coords_lat, mus_lon, mus_lat, 
             w_bf = work.tile([P, PAIRS, width, PACK], BF16, align_bytes=64)
             nc.vector.tensor_tensor(
                 out=w_bf[:],
-                in0=product_tiles.pop(i)[:].rearrange("k j t m -> k j m t"),
+                in0=product_tiles.pop(i)[:],
                 in1=spread_tiles.pop(i)[:].unsqueeze(3).to_broadcast([P, PAIRS, width, PACK]),
                 op=ALU.mult,
             )
@@ -263,14 +278,12 @@ def tile_normal_nolayer_kernel(tc, x, coords_lon, coords_lat, mus_lon, mus_lat, 
                     )
 
         with tc.manual_schedule():
-            for step in range(-1 - AHEAD * BLOCK, CHUNKS + 4):
+            for step in range(-2 - SQ_CHUNKS, CHUNKS + 4):
                 ask = step + 1 + AHEAD * BLOCK
                 if 0 <= ask < CHUNKS and ask % BLOCK == 0:
                     load_x(ask // BLOCK)
-                if 0 <= step + 3 < CHUNKS:
-                    distances(step + 3)
-                if 0 <= step + 2 < CHUNKS:
-                    squares(step + 2)
+                if 0 <= step + 2 + SQ_CHUNKS < CHUNKS:
+                    squares((step + 2 + SQ_CHUNKS) // SQ_CHUNKS, (step + 2 + SQ_CHUNKS) % SQ_CHUNKS)
                 if 0 <= step + 1 < CHUNKS:
                     products_on_gpsimd(step + 1)
                     regroup_x(step + 1)

@@ -26,7 +26,7 @@ BLOCK = 2
 AHEAD = 2
 W_SETS = 3
 RUN = 4
-GP_PAIRS = 3
+GP_PAIRS = 2
 SQ_CHUNKS = 4
 
 FLOPS = 2 * BATCH * NWIN * P * PACK * COLS_X * COLS_W
@@ -135,6 +135,7 @@ def tile_normal_nolayer_kernel(tc, x, coords_lon, coords_lat, mus_lon, mus_lat, 
         x_code_tiles = {}
         x_scale_tiles = {}
         product_tiles = {}
+        gp_product_tiles = {}
         sum_tiles = {}
         spread_tiles = {}
         acc_tiles = {}
@@ -176,28 +177,30 @@ def tile_normal_nolayer_kernel(tc, x, coords_lon, coords_lat, mus_lon, mus_lat, 
             span = chunk_windows(i, first, last)
             count = (last - first) * BATCH
             engine.tensor_tensor(
-                out=g[:, first:last].rearrange("k j (b p q) t -> k (j b) p q t", b=BATCH, p=OFFS),
+                out=g[:].rearrange("k j (b p q) t -> k (j b) p q t", b=BATCH, p=OFFS),
                 in0=gauss[:, 0, span].unsqueeze(3).to_broadcast([P, count, OFFS, OFFS, PACK]),
                 in1=gauss[:, 1, span].unsqueeze(2).to_broadcast([P, count, OFFS, OFFS, PACK]),
                 op=ALU.mult,
             )
 
         def products_on_gpsimd(i):
-            g = work.tile([P, PAIRS, BATCH * COLS_W, PACK], F32, bufs=5)
+            g = work.tile([P, GP_PAIRS, BATCH * COLS_W, PACK], F32, name="g_gpsimd", bufs=3)
             outer_products(nc.gpsimd, g, i, PAIRS - GP_PAIRS, PAIRS)
-            product_tiles[i] = g
+            gp_product_tiles[i] = g
 
         def products(i):
-            g = product_tiles[i]
+            g = work.tile([P, PAIRS - GP_PAIRS, BATCH * COLS_W, PACK], F32, name="g_vector", bufs=3)
             outer_products(nc.vector, g, i, 0, PAIRS - GP_PAIRS)
+            product_tiles[i] = g
             if i % SQ_CHUNKS == SQ_CHUNKS - 1:
                 gauss_tiles.pop(i // SQ_CHUNKS)
             sums = psum.tile([P, PAIRS, P], F32, tag="sums")
             for j in range(PAIRS):
+                source = g[:, j] if j < PAIRS - GP_PAIRS else gp_product_tiles[i][:, j - (PAIRS - GP_PAIRS)]
                 for t in range(PACK):
                     nc.tensor.matmul(
                         out=sums[:, j, :],
-                        lhsT=g[:, j, :, t],
+                        lhsT=source[:, :, t],
                         rhs=ident_f[:],
                         is_transpose=True,
                         start=(t == 0),
@@ -218,16 +221,27 @@ def tile_normal_nolayer_kernel(tc, x, coords_lon, coords_lat, mus_lon, mus_lat, 
                 nc.tensor.transpose(spread[:, j, :], inverse[:, j : j + 1].to_broadcast([P, P]), ident_f[:])
             spread_tiles[i] = spread
 
-        def weights(i):
+        def weights_of_gpsimd(i):
             width = BATCH * COLS_W
             w_bf = work.tile([P, PAIRS, width, PACK], BF16, align_bytes=64)
+            w_tiles[i] = w_bf
+            first = PAIRS - GP_PAIRS
             nc.vector.tensor_tensor(
-                out=w_bf[:],
-                in0=product_tiles.pop(i)[:],
-                in1=spread_tiles.pop(i)[:].unsqueeze(3).to_broadcast([P, PAIRS, width, PACK]),
+                out=w_bf[:, first:],
+                in0=gp_product_tiles.pop(i)[:],
+                in1=spread_tiles[i][:, first:].unsqueeze(3).to_broadcast([P, GP_PAIRS, width, PACK]),
                 op=ALU.mult,
             )
-            w_tiles[i] = w_bf
+
+        def weights_of_vector(i):
+            width = BATCH * COLS_W
+            first = PAIRS - GP_PAIRS
+            nc.vector.tensor_tensor(
+                out=w_tiles[i][:, :first],
+                in0=product_tiles.pop(i)[:],
+                in1=spread_tiles.pop(i)[:, :first].unsqueeze(3).to_broadcast([P, first, width, PACK]),
+                op=ALU.mult,
+            )
 
         def quantise_w(i):
             w_bf = w_tiles.pop(i)
@@ -284,19 +298,21 @@ def tile_normal_nolayer_kernel(tc, x, coords_lon, coords_lat, mus_lon, mus_lat, 
                     load_x(ask // BLOCK)
                 if 0 <= step + 2 + SQ_CHUNKS < CHUNKS:
                     squares((step + 2 + SQ_CHUNKS) // SQ_CHUNKS, (step + 2 + SQ_CHUNKS) % SQ_CHUNKS)
+                if 0 <= step - 2 < CHUNKS:
+                    weights_of_gpsimd(step - 2)
                 if 0 <= step + 1 < CHUNKS:
                     products_on_gpsimd(step + 1)
                     regroup_x(step + 1)
                 if 0 <= step + 2 < CHUNKS:
                     gaussians(step + 2)
+                if 0 <= step - 2 < CHUNKS:
+                    weights_of_vector(step - 2)
                 if 0 <= step - 1 < CHUNKS:
                     totals(step - 1)
                 if 0 <= step < CHUNKS:
                     products(step)
                 if 0 <= step - 1 < CHUNKS:
                     normalisers(step - 1)
-                if 0 <= step - 2 < CHUNKS:
-                    weights(step - 2)
                 if 0 <= step - 1 < CHUNKS:
                     quantise_x(step - 1)
                 if 0 <= step - 2 < CHUNKS:

@@ -194,19 +194,26 @@ def tile_normal_nolayer_kernel(tc, x, coords_lon, coords_lat, mus_lon, mus_lat, 
             product_tiles[i] = g
             if i % SQ_CHUNKS == SQ_CHUNKS - 1:
                 gauss_tiles.pop(i // SQ_CHUNKS)
-            sums = psum.tile([P, PAIRS, P], F32, tag="sums")
-            for j in range(PAIRS):
-                source = g[:, j] if j < PAIRS - GP_PAIRS else gp_product_tiles[i][:, j - (PAIRS - GP_PAIRS)]
+
+        def sum_over_neighbours(i, g, first, last):
+            for j in range(first, last):
                 for t in range(PACK):
                     nc.tensor.matmul(
-                        out=sums[:, j, :],
-                        lhsT=source[:, :, t],
+                        out=sum_tiles[i][:, j, :],
+                        lhsT=g[:, j - first, :, t],
                         rhs=ident_f[:],
                         is_transpose=True,
                         start=(t == 0),
                         stop=(t == PACK - 1),
                     )
+
+        def sums_of_gpsimd(i):
+            sums = psum.tile([P, PAIRS, P], F32, tag="sums")
             sum_tiles[i] = sums
+            sum_over_neighbours(i, gp_product_tiles[i], PAIRS - GP_PAIRS, PAIRS)
+
+        def sums_of_vector(i):
+            sum_over_neighbours(i, product_tiles[i], 0, PAIRS - GP_PAIRS)
 
         def totals(i):
             total = work.tile([P, PAIRS], F32)
@@ -305,6 +312,8 @@ def tile_normal_nolayer_kernel(tc, x, coords_lon, coords_lat, mus_lon, mus_lat, 
                     regroup_x(step + 1)
                 if 0 <= step + 2 < CHUNKS:
                     gaussians(step + 2)
+                if 0 <= step < CHUNKS:
+                    sums_of_gpsimd(step)
                 if 0 <= step - 2 < CHUNKS:
                     weights_of_vector(step - 2)
                 if 0 <= step - 1 < CHUNKS:
@@ -313,6 +322,8 @@ def tile_normal_nolayer_kernel(tc, x, coords_lon, coords_lat, mus_lon, mus_lat, 
                     products(step)
                 if 0 <= step - 1 < CHUNKS:
                     normalisers(step - 1)
+                if 0 <= step < CHUNKS:
+                    sums_of_vector(step)
                 if 0 <= step - 1 < CHUNKS:
                     quantise_x(step - 1)
                 if 0 <= step - 2 < CHUNKS:

@@ -27,6 +27,7 @@ AHEAD = 2
 W_SETS = 3
 RUN = 4
 GP_PAIRS = 2
+HEAD_CHUNKS = 2
 SQ_CHUNKS = 4
 
 FLOPS = 2 * BATCH * NWIN * P * PACK * COLS_X * COLS_W
@@ -155,6 +156,12 @@ def tile_normal_nolayer_kernel(tc, x, coords_lon, coords_lat, mus_lon, mus_lat, 
             first = (i % BLOCK) * PAIRS
             raw = raw_tiles[i // BLOCK]
             for b in range(BATCH):
+                if i < HEAD_CHUNKS:
+                    nc.vector.tensor_copy(
+                        out=grouped[:, b],
+                        in_=raw[:, b, first : first + PAIRS, :].rearrange("k j (t c) -> k j c t", t=PACK),
+                    )
+                    continue
                 nc.scalar.copy(
                     out=grouped[:, b].rearrange("k j (c r) t -> k j c t r", r=RUN),
                     in_=raw[:, b, first : first + PAIRS, :].rearrange("k j (t c r) -> k j c t r", t=PACK, r=RUN),
@@ -250,29 +257,29 @@ def tile_normal_nolayer_kernel(tc, x, coords_lon, coords_lat, mus_lon, mus_lat, 
                 op=ALU.mult,
             )
 
-        def quantise_w(i):
-            w_bf = w_tiles.pop(i)
+        def quantise_w(i, first, last):
+            w_bf = w_tiles[i]
             codes = w_codes[i % W_SETS]
             scales = w_scales[i % W_SETS]
             inner = slice(COLS_W, 3 * COLS_W)
-            for j in range(PAIRS):
+            for j in range(first, last):
                 nc.vector.quantize_mx(
                     out=codes[:, j, inner].bitcast(FP8X4),
                     scales=scales[:, j, inner],
                     in_=w_bf[:, j].rearrange("k m t -> k (m t)"),
                 )
 
-        def contract(i):
+        def contract(i, first, last):
             codes = w_codes[i % W_SETS]
             scales = w_scales[i % W_SETS]
-            x_codes = x_code_tiles.pop(i)
-            x_scales = x_scale_tiles.pop(i)
-            acc = psum.tile([P, PAIRS, COLS_X], F32, tag="acc")
-            for j in range(PAIRS):
+            x_codes = x_code_tiles[i]
+            x_scales = x_scale_tiles[i]
+            acc = psum.tile([P, last - first, COLS_X], F32, tag="acc")
+            for j in range(first, last):
                 for b in range(BATCH):
                     half = slice(b * 2 * COLS_W, (b + 1) * 2 * COLS_W)
                     nc.tensor.matmul_mx(
-                        out=acc[:, j, :],
+                        out=acc[:, j - first, :],
                         lhsT=codes[:, j, half].bitcast(FP8X4),
                         lhsT_scale=scales[:, j, half],
                         rhs=x_codes[:, b, j, :].bitcast(FP8X4),
@@ -282,24 +289,33 @@ def tile_normal_nolayer_kernel(tc, x, coords_lon, coords_lat, mus_lon, mus_lat, 
                     )
             acc_tiles[i] = acc
 
+        def send(result, first_pair, count):
+            per_pair = COLS_X // CHAN
+            for b in range(BATCH):
+                lanes = slice((1 - b) * COLS_W, (2 - b) * COLS_W)
+                nc.sync.dma_start(
+                    out=out_view[b, :, first_pair * per_pair : (first_pair + count) * per_pair, :],
+                    in_=result[lanes].rearrange("m j (v c) -> m (j v) c", c=CHAN),
+                )
+
         def store(i):
             block = i // BLOCK
             if i % BLOCK == 0:
-                result = work.tile([P, BLOCK, PAIRS, COLS_X], F32)
+                result = work.tile([P, BLOCK * PAIRS, COLS_X], F32)
                 result_tiles[block] = result
             result = result_tiles[block]
-            nc.scalar.copy(out=result[:, i % BLOCK], in_=acc_tiles.pop(i)[:])
+            slot = (i % BLOCK) * PAIRS
+            nc.scalar.copy(out=result[:, slot : slot + PAIRS], in_=acc_tiles.pop(i)[:])
             if i % BLOCK == BLOCK - 1:
-                rows_nv = BLOCK * PAIRS * (COLS_X // CHAN)
-                for b in range(BATCH):
-                    lanes = slice((1 - b) * COLS_W, (2 - b) * COLS_W)
-                    nc.sync.dma_start(
-                        out=out_view[b, :, block * rows_nv : (block + 1) * rows_nv, :],
-                        in_=result[lanes].rearrange("m u j (v c) -> m (u j v) c", c=CHAN),
-                    )
+                send(result[:], block * BLOCK * PAIRS, BLOCK * PAIRS)
+
+        def store_at_once(i, first, last):
+            part = work.tile([P, last - first, COLS_X], F32, name="part", bufs=3)
+            nc.scalar.copy(out=part[:], in_=acc_tiles.pop(i)[:])
+            send(part[:], i * PAIRS + first, last - first)
 
         with tc.manual_schedule():
-            for step in range(-2 - SQ_CHUNKS, CHUNKS + 4):
+            for step in range(-2 - SQ_CHUNKS, CHUNKS + 1):
                 ask = step + 1 + AHEAD * BLOCK
                 if 0 <= ask < CHUNKS and ask % BLOCK == 0:
                     load_x(ask // BLOCK)
@@ -327,7 +343,14 @@ def tile_normal_nolayer_kernel(tc, x, coords_lon, coords_lat, mus_lon, mus_lat, 
                 if 0 <= step - 1 < CHUNKS:
                     quantise_x(step - 1)
                 if 0 <= step - 2 < CHUNKS:
-                    quantise_w(step - 2)
-                    contract(step - 2)
+                    quantise_w(step - 2, 0, PAIRS)
+                    contract(step - 2, 0, PAIRS)
                 if 0 <= step - 3 < CHUNKS:
                     store(step - 3)
+            store_at_once(CHUNKS - 2, 0, PAIRS)
+            weights_of_gpsimd(CHUNKS - 1)
+            weights_of_vector(CHUNKS - 1)
+            for first in (PAIRS - GP_PAIRS, 0):
+                quantise_w(CHUNKS - 1, first, first + PAIRS // 2)
+                contract(CHUNKS - 1, first, first + PAIRS // 2)
+                store_at_once(CHUNKS - 1, first, first + PAIRS // 2)

@@ -27,7 +27,6 @@ AHEAD = 2
 W_SETS = 3
 RUN = 4
 GP_PAIRS = 2
-HEAD_CHUNKS = 2
 SQ_CHUNKS = 4
 
 FLOPS = 2 * BATCH * NWIN * P * PACK * COLS_X * COLS_W
@@ -156,12 +155,6 @@ def tile_normal_nolayer_kernel(tc, x, coords_lon, coords_lat, mus_lon, mus_lat, 
             first = (i % BLOCK) * PAIRS
             raw = raw_tiles[i // BLOCK]
             for b in range(BATCH):
-                if i < HEAD_CHUNKS:
-                    nc.vector.tensor_copy(
-                        out=grouped[:, b],
-                        in_=raw[:, b, first : first + PAIRS, :].rearrange("k j (t c) -> k j c t", t=PACK),
-                    )
-                    continue
                 nc.scalar.copy(
                     out=grouped[:, b].rearrange("k j (c r) t -> k j c t r", r=RUN),
                     in_=raw[:, b, first : first + PAIRS, :].rearrange("k j (t c r) -> k j c t r", t=PACK, r=RUN),

@@ -27,6 +27,8 @@ AHEAD = 2
 W_SETS = 3
 RUN = 4
 GP_PAIRS = 2
+SHARED = 5
+HEAD_CHUNKS = 2
 SQ_CHUNKS = 4
 
 FLOPS = 2 * BATCH * NWIN * P * PACK * COLS_X * COLS_W
@@ -83,6 +85,11 @@ def tile_normal_nolayer_kernel(tc, x, coords_lon, coords_lat, mus_lon, mus_lat, 
             scales = keep.tile([P, PAIRS, 4 * COLS_W], U8, name="w_scales%d" % i, align_bytes=64)
             nc.vector.memset(scales[:].bitcast(I32), 0)
             w_scales.append(scales)
+
+        shared = []
+        for i in range(SHARED):
+            shared_tile = keep.tile([P, GP_PAIRS * BATCH * COLS_W * PACK], F32, name="shared%d" % i, align_bytes=64)
+            shared.append(shared_tile)
 
         coord = keep.tile([P, 2, NWIN, BATCH, PACK], BF16)
         for a in range(2):
@@ -155,6 +162,12 @@ def tile_normal_nolayer_kernel(tc, x, coords_lon, coords_lat, mus_lon, mus_lat, 
             first = (i % BLOCK) * PAIRS
             raw = raw_tiles[i // BLOCK]
             for b in range(BATCH):
+                if i < HEAD_CHUNKS:
+                    nc.vector.tensor_copy(
+                        out=grouped[:, b],
+                        in_=raw[:, b, first : first + PAIRS, :].rearrange("k j (t c) -> k j c t", t=PACK),
+                    )
+                    continue
                 nc.scalar.copy(
                     out=grouped[:, b].rearrange("k j (c r) t -> k j c t r", r=RUN),
                     in_=raw[:, b, first : first + PAIRS, :].rearrange("k j (t c r) -> k j c t r", t=PACK, r=RUN),
@@ -177,20 +190,20 @@ def tile_normal_nolayer_kernel(tc, x, coords_lon, coords_lat, mus_lon, mus_lat, 
             span = chunk_windows(i, first, last)
             count = (last - first) * BATCH
             engine.tensor_tensor(
-                out=g[:].rearrange("k j (b p q) t -> k (j b) p q t", b=BATCH, p=OFFS),
+                out=g.rearrange("k j (b p q) t -> k (j b) p q t", b=BATCH, p=OFFS),
                 in0=gauss[:, 0, span].unsqueeze(3).to_broadcast([P, count, OFFS, OFFS, PACK]),
                 in1=gauss[:, 1, span].unsqueeze(2).to_broadcast([P, count, OFFS, OFFS, PACK]),
                 op=ALU.mult,
             )
 
         def products_on_gpsimd(i):
-            g = work.tile([P, GP_PAIRS, BATCH * COLS_W, PACK], F32, name="g_gpsimd", bufs=3)
+            g = shared[(i - 2) % SHARED][:].rearrange("k (j m t) -> k j m t", j=GP_PAIRS, t=PACK)
             outer_products(nc.gpsimd, g, i, PAIRS - GP_PAIRS, PAIRS)
             gp_product_tiles[i] = g
 
         def products(i):
             g = work.tile([P, PAIRS - GP_PAIRS, BATCH * COLS_W, PACK], F32, name="g_vector", bufs=3)
-            outer_products(nc.vector, g, i, 0, PAIRS - GP_PAIRS)
+            outer_products(nc.vector, g[:], i, 0, PAIRS - GP_PAIRS)
             product_tiles[i] = g
             if i % SQ_CHUNKS == SQ_CHUNKS - 1:
                 gauss_tiles.pop(i // SQ_CHUNKS)
@@ -230,12 +243,12 @@ def tile_normal_nolayer_kernel(tc, x, coords_lon, coords_lat, mus_lon, mus_lat, 
 
         def weights_of_gpsimd(i):
             width = BATCH * COLS_W
-            w_bf = work.tile([P, PAIRS, width, PACK], BF16, align_bytes=64)
+            w_bf = shared[(i + 2) % SHARED][:].bitcast(BF16).rearrange("k (j m t) -> k j m t", j=PAIRS, t=PACK)
             w_tiles[i] = w_bf
             first = PAIRS - GP_PAIRS
             nc.vector.tensor_tensor(
                 out=w_bf[:, first:],
-                in0=gp_product_tiles.pop(i)[:],
+                in0=gp_product_tiles.pop(i),
                 in1=spread_tiles[i][:, first:].unsqueeze(3).to_broadcast([P, GP_PAIRS, width, PACK]),
                 op=ALU.mult,
             )
@@ -308,19 +321,18 @@ def tile_normal_nolayer_kernel(tc, x, coords_lon, coords_lat, mus_lon, mus_lat, 
             send(part[:], i * PAIRS + first, last - first)
 
         with tc.manual_schedule():
-            for step in range(-2 - SQ_CHUNKS, CHUNKS + 1):
+            for step in range(-3 - SQ_CHUNKS, CHUNKS + 1):
                 ask = step + 1 + AHEAD * BLOCK
                 if 0 <= ask < CHUNKS and ask % BLOCK == 0:
                     load_x(ask // BLOCK)
-                if 0 <= step + 2 + SQ_CHUNKS < CHUNKS:
-                    squares((step + 2 + SQ_CHUNKS) // SQ_CHUNKS, (step + 2 + SQ_CHUNKS) % SQ_CHUNKS)
+                if 0 <= step + 3 + SQ_CHUNKS < CHUNKS:
+                    squares((step + 3 + SQ_CHUNKS) // SQ_CHUNKS, (step + 3 + SQ_CHUNKS) % SQ_CHUNKS)
                 if 0 <= step - 2 < CHUNKS:
                     weights_of_gpsimd(step - 2)
                 if 0 <= step + 1 < CHUNKS:
-                    products_on_gpsimd(step + 1)
                     regroup_x(step + 1)
-                if 0 <= step + 2 < CHUNKS:
-                    gaussians(step + 2)
+                if 0 <= step + 3 < CHUNKS:
+                    gaussians(step + 3)
                 if 0 <= step < CHUNKS:
                     sums_of_gpsimd(step)
                 if 0 <= step - 2 < CHUNKS:
@@ -338,6 +350,8 @@ def tile_normal_nolayer_kernel(tc, x, coords_lon, coords_lat, mus_lon, mus_lat, 
                 if 0 <= step - 2 < CHUNKS:
                     quantise_w(step - 2, 0, PAIRS)
                     contract(step - 2, 0, PAIRS)
+                if 0 <= step + 2 < CHUNKS:
+                    products_on_gpsimd(step + 2)
                 if 0 <= step - 3 < CHUNKS:
                     store(step - 3)
             store_at_once(CHUNKS - 2, 0, PAIRS)

@@ -29,6 +29,7 @@ RUN = 4
 GP_PAIRS = 2
 SHARED = 5
 HEAD_CHUNKS = 2
+BANK = 512
 SQ_CHUNKS = 4
 
 FLOPS = 2 * BATCH * NWIN * P * PACK * COLS_X * COLS_W
@@ -143,6 +144,7 @@ def tile_normal_nolayer_kernel(tc, x, coords_lon, coords_lat, mus_lon, mus_lat, 
         x_scale_tiles = {}
         product_tiles = {}
         gp_product_tiles = {}
+        lon_tiles = {}
         sum_tiles = {}
         spread_tiles = {}
         acc_tiles = {}
@@ -201,9 +203,32 @@ def tile_normal_nolayer_kernel(tc, x, coords_lon, coords_lat, mus_lon, mus_lat, 
             outer_products(nc.gpsimd, g, i, PAIRS - GP_PAIRS, PAIRS)
             gp_product_tiles[i] = g
 
+        def lon_to_psum(i):
+            lon = psum.tile([P, BANK], F32, tag="lon")
+            count = (PAIRS - GP_PAIRS) * BATCH
+            nc.tensor.matmul(
+                out=lon[:, : count * OFFS * PACK],
+                lhsT=ident_f[:],
+                rhs=gauss_tiles[i // SQ_CHUNKS][:, 0, chunk_windows(i, 0, PAIRS - GP_PAIRS)].rearrange("k w p t -> k (w p t)"),
+                start=True,
+                stop=True,
+            )
+            lon_tiles[i] = lon
+
         def products(i):
             g = work.tile([P, PAIRS - GP_PAIRS, BATCH * COLS_W, PACK], F32, name="g_vector", bufs=3)
-            outer_products(nc.vector, g[:], i, 0, PAIRS - GP_PAIRS)
+            count = (PAIRS - GP_PAIRS) * BATCH
+            nc.vector.tensor_tensor(
+                out=g[:].rearrange("k j (b p q) t -> k (j b) p q t", b=BATCH, p=OFFS),
+                in0=lon_tiles.pop(i)[:, : count * OFFS * PACK]
+                .rearrange("k (w p t) -> k w p t", p=OFFS, t=PACK)
+                .unsqueeze(3)
+                .to_broadcast([P, count, OFFS, OFFS, PACK]),
+                in1=gauss_tiles[i // SQ_CHUNKS][:, 1, chunk_windows(i, 0, PAIRS - GP_PAIRS)]
+                .unsqueeze(2)
+                .to_broadcast([P, count, OFFS, OFFS, PACK]),
+                op=ALU.mult,
+            )
             product_tiles[i] = g
             if i % SQ_CHUNKS == SQ_CHUNKS - 1:
                 gauss_tiles.pop(i // SQ_CHUNKS)
@@ -334,6 +359,7 @@ def tile_normal_nolayer_kernel(tc, x, coords_lon, coords_lat, mus_lon, mus_lat, 
                 if 0 <= step + 3 < CHUNKS:
                     gaussians(step + 3)
                 if 0 <= step < CHUNKS:
+                    lon_to_psum(step)
                     sums_of_gpsimd(step)
                 if 0 <= step - 2 < CHUNKS:
                     weights_of_vector(step - 2)

@@ -26,7 +26,7 @@ BLOCK = 2
 AHEAD = 2
 W_SETS = 3
 RUN = 4
-GP_PAIRS = 2
+GP_PAIRS = 3
 SHARED = 5
 HEAD_CHUNKS = 2
 BANK = 512
@@ -268,7 +268,11 @@ def tile_normal_nolayer_kernel(tc, x, coords_lon, coords_lat, mus_lon, mus_lat, 
 
         def weights_of_gpsimd(i):
             width = BATCH * COLS_W
-            w_bf = shared[(i + 2) % SHARED][:].bitcast(BF16).rearrange("k (j m t) -> k j m t", j=PAIRS, t=PACK)
+            w_bf = (
+                shared[(i + 2) % SHARED][:, : PAIRS * width * PACK // 2]
+                .bitcast(BF16)
+                .rearrange("k (j m t) -> k j m t", j=PAIRS, t=PACK)
+            )
             w_tiles[i] = w_bf
             first = PAIRS - GP_PAIRS
             nc.vector.tensor_tensor(
@@ -383,7 +387,7 @@ def tile_normal_nolayer_kernel(tc, x, coords_lon, coords_lat, mus_lon, mus_lat, 
             store_at_once(CHUNKS - 2, 0, PAIRS)
             weights_of_gpsimd(CHUNKS - 1)
             weights_of_vector(CHUNKS - 1)
-            for first in (PAIRS - GP_PAIRS, 0):
+            for first in (PAIRS // 2, 0):
                 quantise_w(CHUNKS - 1, first, first + PAIRS // 2)
                 contract(CHUNKS - 1, first, first + PAIRS // 2)
                 store_at_once(CHUNKS - 1, first, first + PAIRS // 2)

@@ -26,7 +26,8 @@ BLOCK = 2
 AHEAD = 2
 W_SETS = 3
 RUN = 4
-GP_PAIRS = 3
+WINDOWS = PAIRS * BATCH
+GP_WINDOWS = 5
 SHARED = 5
 HEAD_CHUNKS = 2
 BANK = 512
@@ -89,7 +90,7 @@ def tile_normal_nolayer_kernel(tc, x, coords_lon, coords_lat, mus_lon, mus_lat, 
 
         shared = []
         for i in range(SHARED):
-            shared_tile = keep.tile([P, GP_PAIRS * BATCH * COLS_W * PACK], F32, name="shared%d" % i, align_bytes=64)
+            shared_tile = keep.tile([P, WINDOWS * COLS_W * PACK], F32, name="shared%d" % i, align_bytes=64)
             shared.append(shared_tile)
 
         coord = keep.tile([P, 2, NWIN, BATCH, PACK], BF16)
@@ -109,13 +110,11 @@ def tile_normal_nolayer_kernel(tc, x, coords_lon, coords_lat, mus_lon, mus_lat, 
                     in_=turned[:, :, first_col : first_col + NWIN].rearrange("k t n -> k n t"),
                 )
 
-        windows = PAIRS * BATCH
-
         gauss_tiles = {}
 
         def squares(group, part):
             if part == 0:
-                new_tile = work.tile([P, 2, SQ_CHUNKS * windows, OFFS, PACK], F32, name="gauss", bufs=3)
+                new_tile = work.tile([P, 2, SQ_CHUNKS * WINDOWS, OFFS, PACK], F32, name="gauss", bufs=3)
                 gauss_tiles[group] = new_tile
             gauss = gauss_tiles[group]
             pairs = slice(group * SQ_CHUNKS * PAIRS, (group + 1) * SQ_CHUNKS * PAIRS)
@@ -131,11 +130,11 @@ def tile_normal_nolayer_kernel(tc, x, coords_lon, coords_lat, mus_lon, mus_lat, 
                 )
 
         def chunk_windows(i, first, last):
-            start = (i % SQ_CHUNKS) * windows
-            return slice(start + first * BATCH, start + last * BATCH)
+            start = (i % SQ_CHUNKS) * WINDOWS
+            return slice(start + first, start + last)
 
         def gaussians(i):
-            part = gauss_tiles[i // SQ_CHUNKS][:, :, chunk_windows(i, 0, PAIRS)]
+            part = gauss_tiles[i // SQ_CHUNKS][:, :, chunk_windows(i, 0, WINDOWS)]
             nc.scalar.activation(out=part, in_=part, func=ACT.Exp, scale=-0.5)
 
         raw_tiles = {}
@@ -143,7 +142,6 @@ def tile_normal_nolayer_kernel(tc, x, coords_lon, coords_lat, mus_lon, mus_lat, 
         x_code_tiles = {}
         x_scale_tiles = {}
         product_tiles = {}
-        gp_product_tiles = {}
         lon_tiles = {}
         sum_tiles = {}
         spread_tiles = {}
@@ -187,58 +185,52 @@ def tile_normal_nolayer_kernel(tc, x, coords_lon, coords_lat, mus_lon, mus_lat, 
             x_code_tiles[i] = x_codes
             x_scale_tiles[i] = x_scales
 
-        def outer_products(engine, g, i, first, last):
+        def products_on_gpsimd(i):
+            g = shared[(i - 2) % SHARED][:].rearrange("k (w m t) -> k w m t", w=WINDOWS, t=PACK)
             gauss = gauss_tiles[i // SQ_CHUNKS]
-            span = chunk_windows(i, first, last)
-            count = (last - first) * BATCH
-            engine.tensor_tensor(
-                out=g.rearrange("k j (b p q) t -> k (j b) p q t", b=BATCH, p=OFFS),
-                in0=gauss[:, 0, span].unsqueeze(3).to_broadcast([P, count, OFFS, OFFS, PACK]),
-                in1=gauss[:, 1, span].unsqueeze(2).to_broadcast([P, count, OFFS, OFFS, PACK]),
+            span = chunk_windows(i, 0, GP_WINDOWS)
+            nc.gpsimd.tensor_tensor(
+                out=g[:, :GP_WINDOWS].rearrange("k w (p q) t -> k w p q t", p=OFFS),
+                in0=gauss[:, 0, span].unsqueeze(3).to_broadcast([P, GP_WINDOWS, OFFS, OFFS, PACK]),
+                in1=gauss[:, 1, span].unsqueeze(2).to_broadcast([P, GP_WINDOWS, OFFS, OFFS, PACK]),
                 op=ALU.mult,
             )
-
-        def products_on_gpsimd(i):
-            g = shared[(i - 2) % SHARED][:].rearrange("k (j m t) -> k j m t", j=GP_PAIRS, t=PACK)
-            outer_products(nc.gpsimd, g, i, PAIRS - GP_PAIRS, PAIRS)
-            gp_product_tiles[i] = g
+            product_tiles[i] = g
 
         def lon_to_psum(i):
             lon = psum.tile([P, BANK], F32, tag="lon")
-            count = (PAIRS - GP_PAIRS) * BATCH
             nc.tensor.matmul(
-                out=lon[:, : count * OFFS * PACK],
+                out=lon[:, : (WINDOWS - GP_WINDOWS) * OFFS * PACK],
                 lhsT=ident_f[:],
-                rhs=gauss_tiles[i // SQ_CHUNKS][:, 0, chunk_windows(i, 0, PAIRS - GP_PAIRS)].rearrange("k w p t -> k (w p t)"),
+                rhs=gauss_tiles[i // SQ_CHUNKS][:, 0, chunk_windows(i, GP_WINDOWS, WINDOWS)].rearrange("k w p t -> k (w p t)"),
                 start=True,
                 stop=True,
             )
             lon_tiles[i] = lon
 
         def products(i):
-            g = work.tile([P, PAIRS - GP_PAIRS, BATCH * COLS_W, PACK], F32, name="g_vector", bufs=3)
-            count = (PAIRS - GP_PAIRS) * BATCH
+            count = WINDOWS - GP_WINDOWS
             nc.vector.tensor_tensor(
-                out=g[:].rearrange("k j (b p q) t -> k (j b) p q t", b=BATCH, p=OFFS),
+                out=product_tiles[i][:, GP_WINDOWS:].rearrange("k w (p q) t -> k w p q t", p=OFFS),
                 in0=lon_tiles.pop(i)[:, : count * OFFS * PACK]
                 .rearrange("k (w p t) -> k w p t", p=OFFS, t=PACK)
                 .unsqueeze(3)
                 .to_broadcast([P, count, OFFS, OFFS, PACK]),
-                in1=gauss_tiles[i // SQ_CHUNKS][:, 1, chunk_windows(i, 0, PAIRS - GP_PAIRS)]
+                in1=gauss_tiles[i // SQ_CHUNKS][:, 1, chunk_windows(i, GP_WINDOWS, WINDOWS)]
                 .unsqueeze(2)
                 .to_broadcast([P, count, OFFS, OFFS, PACK]),
                 op=ALU.mult,
             )
-            product_tiles[i] = g
             if i % SQ_CHUNKS == SQ_CHUNKS - 1:
                 gauss_tiles.pop(i // SQ_CHUNKS)
 
-        def sum_over_neighbours(i, g, first, last):
+        def sum_over_neighbours(i, first, last):
+            g = product_tiles[i].rearrange("k (j b) m t -> k j (b m) t", b=BATCH)
             for j in range(first, last):
                 for t in range(PACK):
                     nc.tensor.matmul(
                         out=sum_tiles[i][:, j, :],
-                        lhsT=g[:, j - first, :, t],
+                        lhsT=g[:, j, :, t],
                         rhs=ident_f[:],
                         is_transpose=True,
                         start=(t == 0),
@@ -248,10 +240,10 @@ def tile_normal_nolayer_kernel(tc, x, coords_lon, coords_lat, mus_lon, mus_lat, 
         def sums_of_gpsimd(i):
             sums = psum.tile([P, PAIRS, P], F32, tag="sums")
             sum_tiles[i] = sums
-            sum_over_neighbours(i, gp_product_tiles[i], PAIRS - GP_PAIRS, PAIRS)
+            sum_over_neighbours(i, 0, GP_WINDOWS // BATCH)
 
         def sums_of_vector(i):
-            sum_over_neighbours(i, product_tiles[i], 0, PAIRS - GP_PAIRS)
+            sum_over_neighbours(i, GP_WINDOWS // BATCH, PAIRS)
 
         def totals(i):
             total = work.tile([P, PAIRS], F32)
@@ -266,29 +258,14 @@ def tile_normal_nolayer_kernel(tc, x, coords_lon, coords_lat, mus_lon, mus_lat, 
                 nc.tensor.transpose(spread[:, j, :], inverse[:, j : j + 1].to_broadcast([P, P]), ident_f[:])
             spread_tiles[i] = spread
 
-        def weights_of_gpsimd(i):
-            width = BATCH * COLS_W
-            w_bf = (
-                shared[(i + 2) % SHARED][:, : PAIRS * width * PACK // 2]
-                .bitcast(BF16)
-                .rearrange("k (j m t) -> k j m t", j=PAIRS, t=PACK)
-            )
-            w_tiles[i] = w_bf
-            first = PAIRS - GP_PAIRS
+        def weights(i):
+            width = WINDOWS * COLS_W
+            w_bf = shared[(i + 2) % SHARED][:, : width * PACK // 2].bitcast(BF16)
+            w_tiles[i] = w_bf.rearrange("k (j m t) -> k j m t", j=PAIRS, t=PACK)
             nc.vector.tensor_tensor(
-                out=w_bf[:, first:],
-                in0=gp_product_tiles.pop(i),
-                in1=spread_tiles[i][:, first:].unsqueeze(3).to_broadcast([P, GP_PAIRS, width, PACK]),
-                op=ALU.mult,
-            )
-
-        def weights_of_vector(i):
-            width = BATCH * COLS_W
-            first = PAIRS - GP_PAIRS
-            nc.vector.tensor_tensor(
-                out=w_tiles[i][:, :first],
-                in0=product_tiles.pop(i)[:],
-                in1=spread_tiles.pop(i)[:, :first].unsqueeze(3).to_broadcast([P, first, width, PACK]),
+                out=w_bf.rearrange("k (m t) -> k m t", t=PACK),
+                in0=product_tiles.pop(i).rearrange("k w m t -> k (w m) t"),
+                in1=spread_tiles.pop(i)[:].rearrange("k j m -> k (j m)").unsqueeze(2).to_broadcast([P, width, PACK]),
                 op=ALU.mult,
             )
 
@@ -357,7 +334,7 @@ def tile_normal_nolayer_kernel(tc, x, coords_lon, coords_lat, mus_lon, mus_lat, 
                 if 0 <= step + 3 + SQ_CHUNKS < CHUNKS:
                     squares((step + 3 + SQ_CHUNKS) // SQ_CHUNKS, (step + 3 + SQ_CHUNKS) % SQ_CHUNKS)
                 if 0 <= step - 2 < CHUNKS:
-                    weights_of_gpsimd(step - 2)
+                    weights(step - 2)
                 if 0 <= step + 1 < CHUNKS:
                     regroup_x(step + 1)
                 if 0 <= step + 3 < CHUNKS:
@@ -365,8 +342,6 @@ def tile_normal_nolayer_kernel(tc, x, coords_lon, coords_lat, mus_lon, mus_lat, 
                 if 0 <= step < CHUNKS:
                     lon_to_psum(step)
                     sums_of_gpsimd(step)
-                if 0 <= step - 2 < CHUNKS:
-                    weights_of_vector(step - 2)
                 if 0 <= step - 1 < CHUNKS:
                     totals(step - 1)
                 if 0 <= step < CHUNKS:
@@ -385,8 +360,7 @@ def tile_normal_nolayer_kernel(tc, x, coords_lon, coords_lat, mus_lon, mus_lat, 
                 if 0 <= step - 3 < CHUNKS:
                     store(step - 3)
             store_at_once(CHUNKS - 2, 0, PAIRS)
-            weights_of_gpsimd(CHUNKS - 1)
-            weights_of_vector(CHUNKS - 1)
+            weights(CHUNKS - 1)
             for first in (PAIRS // 2, 0):
                 quantise_w(CHUNKS - 1, first, first + PAIRS // 2)
                 contract(CHUNKS - 1, first, first + PAIRS // 2)

@@ -23,7 +23,7 @@ MIN_SIGMA = 1e-10
 PAIRS = 4
 CHUNKS = NWIN // PAIRS
 BLOCK = 2
-AHEAD = 2
+AHEAD = 3
 W_SETS = 3
 RUN = 4
 WINDOWS = PAIRS * BATCH
@@ -153,8 +153,9 @@ def tile_normal_nolayer_kernel(tc, x, coords_lon, coords_lat, mus_lon, mus_lat, 
         def load_x(block):
             raw = xin.tile([P, BATCH, BLOCK * PAIRS, PACK * COLS_X], BF16)
             pairs = slice(block * BLOCK * PAIRS, (block + 1) * BLOCK * PAIRS)
+            queue = nc.sync if block < AHEAD else nc.scalar
             for b in range(BATCH):
-                nc.sync.dma_start(out=raw[:, b], in_=x_view[b, :, pairs, :])
+                queue.dma_start(out=raw[:, b], in_=x_view[b, :, pairs, :])
             raw_tiles[block] = raw
 
         def regroup_x(i):

@@ -28,6 +28,7 @@ W_SETS = 3
 RUN = 4
 WINDOWS = PAIRS * BATCH
 GP_WINDOWS = 5
+GP_WINDOWS_0 = 3
 SHARED = 5
 HEAD_CHUNKS = 2
 BANK = 512
@@ -78,14 +79,17 @@ def tile_normal_nolayer_kernel(tc, x, coords_lon, coords_lat, mus_lon, mus_lat, 
             )
             neg_mu.append(shifted)
 
+        def outer_columns(words):
+            return words.rearrange("k j (e m) -> k j e m", e=4)[:, :, 0:4:3]
+
         w_codes = []
         w_scales = []
         for i in range(W_SETS):
             codes = keep.tile([P, PAIRS, 4 * COLS_W], U32, name="w_codes%d" % i, align_bytes=64)
-            nc.vector.memset(codes[:].bitcast(I32), 0)
+            nc.vector.memset(outer_columns(codes[:].bitcast(I32)), 0)
             w_codes.append(codes)
             scales = keep.tile([P, PAIRS, 4 * COLS_W], U8, name="w_scales%d" % i, align_bytes=64)
-            nc.vector.memset(scales[:].bitcast(I32), 0)
+            nc.vector.memset(outer_columns(scales[:].bitcast(I32)), 0)
             w_scales.append(scales)
 
         shared = []
@@ -94,40 +98,55 @@ def tile_normal_nolayer_kernel(tc, x, coords_lon, coords_lat, mus_lon, mus_lat, 
             shared.append(shared_tile)
 
         coord = keep.tile([P, 2, NWIN, BATCH, PACK], BF16)
-        for a in range(2):
-            for b in range(BATCH):
-                first_row = b * (BATCH * NWIN - P)
-                first_col = b * (P - NWIN)
-                rows = head.tile([P, P * PACK], BF16, name="rows%d%d" % (a, b))
-                nc.sync.dma_start(out=rows[:], in_=coord_rows[a][first_row : first_row + P, :])
-                sorted_rows = head.tile([P, PACK, P], BF16, name="sorted%d%d" % (a, b))
-                nc.vector.tensor_copy(out=sorted_rows[:], in_=rows[:].rearrange("w (i t) -> w t i", t=PACK))
-                turned = psum.tile([P, PACK, P], BF16, tag="spread")
-                for t in range(PACK):
-                    nc.tensor.transpose(turned[:, t, :], sorted_rows[:, t, :], ident_bf[:])
-                nc.vector.tensor_copy(
-                    out=coord[:, a, :, b, :],
-                    in_=turned[:, :, first_col : first_col + NWIN].rearrange("k t n -> k n t"),
-                )
+
+        def load_coordinates():
+            row_tiles = []
+            for a in range(2):
+                for b in range(BATCH):
+                    first_row = b * (BATCH * NWIN - P)
+                    rows = head.tile([P, P * PACK], BF16, name="rows%d%d" % (a, b))
+                    nc.sync.dma_start(out=rows[:], in_=coord_rows[a][first_row : first_row + P, :])
+                    row_tiles.append(rows)
+            return row_tiles
+
+        def turn_coordinates(row_tiles):
+            for a in range(2):
+                for b in range(BATCH):
+                    by_t = row_tiles[a * BATCH + b][:].rearrange("w (i t) -> w t i", t=PACK)
+                    turned = psum.tile([P, PACK, P], BF16, tag=("spread", "sums")[a])
+                    for t in range(PACK):
+                        nc.tensor.transpose(turned[:, t, :], by_t[:, t, :], ident_bf[:])
+                    first_col = b * (P - NWIN)
+                    nc.vector.tensor_copy(
+                        out=coord[:, a, :, b, :],
+                        in_=turned[:, :, first_col : first_col + NWIN].rearrange("k t n -> k n t"),
+                    )
 
         gauss_tiles = {}
 
-        def squares(group, part):
-            if part == 0:
-                new_tile = work.tile([P, 2, SQ_CHUNKS * WINDOWS, OFFS, PACK], F32, name="gauss", bufs=3)
-                gauss_tiles[group] = new_tile
-            gauss = gauss_tiles[group]
-            pairs = slice(group * SQ_CHUNKS * PAIRS, (group + 1) * SQ_CHUNKS * PAIRS)
-            share = 2 * OFFS // SQ_CHUNKS
-            for number in range(part * share, (part + 1) * share):
+        def open_group(group):
+            new_tile = work.tile([P, 2, SQ_CHUNKS * WINDOWS, OFFS, PACK], F32, name="gauss", bufs=3)
+            gauss_tiles[group] = new_tile
+
+        def squares(group, first, last, numbers):
+            start = group * SQ_CHUNKS
+            pairs = slice((start + first) * PAIRS, (start + last) * PAIRS)
+            for number in numbers:
                 a, o = divmod(number, OFFS)
                 nc.scalar.activation(
-                    out=gauss[:, a, :, o, :],
+                    out=gauss_tiles[group][:, a, first * WINDOWS : last * WINDOWS, o, :],
                     in_=coord[:, a, pairs].rearrange("k n b t -> k (n b) t"),
                     func=ACT.Square,
                     scale=inv_sig[:],
                     bias=neg_mu[a][:, o : o + 1],
                 )
+
+        def quarter_of_squares(quarter):
+            group, part = divmod(quarter, SQ_CHUNKS)
+            if part == 0:
+                open_group(group)
+            share = 2 * OFFS // SQ_CHUNKS
+            squares(group, 0, SQ_CHUNKS, range(part * share, (part + 1) * share))
 
         def chunk_windows(i, first, last):
             start = (i % SQ_CHUNKS) * WINDOWS
@@ -153,7 +172,7 @@ def tile_normal_nolayer_kernel(tc, x, coords_lon, coords_lat, mus_lon, mus_lat, 
         def load_x(block):
             raw = xin.tile([P, BATCH, BLOCK * PAIRS, PACK * COLS_X], BF16)
             pairs = slice(block * BLOCK * PAIRS, (block + 1) * BLOCK * PAIRS)
-            queue = nc.sync if block < AHEAD else nc.scalar
+            queue = nc.sync if block <= AHEAD else nc.scalar
             for b in range(BATCH):
                 queue.dma_start(out=raw[:, b], in_=x_view[b, :, pairs, :])
             raw_tiles[block] = raw
@@ -186,14 +205,18 @@ def tile_normal_nolayer_kernel(tc, x, coords_lon, coords_lat, mus_lon, mus_lat, 
             x_code_tiles[i] = x_codes
             x_scale_tiles[i] = x_scales
 
+        def gp_windows(i):
+            return GP_WINDOWS_0 if i == 0 else GP_WINDOWS
+
         def products_on_gpsimd(i):
             g = shared[(i - 2) % SHARED][:].rearrange("k (w m t) -> k w m t", w=WINDOWS, t=PACK)
             gauss = gauss_tiles[i // SQ_CHUNKS]
-            span = chunk_windows(i, 0, GP_WINDOWS)
+            count = gp_windows(i)
+            span = chunk_windows(i, 0, count)
             nc.gpsimd.tensor_tensor(
-                out=g[:, :GP_WINDOWS].rearrange("k w (p q) t -> k w p q t", p=OFFS),
-                in0=gauss[:, 0, span].unsqueeze(3).to_broadcast([P, GP_WINDOWS, OFFS, OFFS, PACK]),
-                in1=gauss[:, 1, span].unsqueeze(2).to_broadcast([P, GP_WINDOWS, OFFS, OFFS, PACK]),
+                out=g[:, :count].rearrange("k w (p q) t -> k w p q t", p=OFFS),
+                in0=gauss[:, 0, span].unsqueeze(3).to_broadcast([P, count, OFFS, OFFS, PACK]),
+                in1=gauss[:, 1, span].unsqueeze(2).to_broadcast([P, count, OFFS, OFFS, PACK]),
                 op=ALU.mult,
             )
             product_tiles[i] = g
@@ -201,23 +224,23 @@ def tile_normal_nolayer_kernel(tc, x, coords_lon, coords_lat, mus_lon, mus_lat, 
         def lon_to_psum(i):
             lon = psum.tile([P, BANK], F32, tag="lon")
             nc.tensor.matmul(
-                out=lon[:, : (WINDOWS - GP_WINDOWS) * OFFS * PACK],
+                out=lon[:, : (WINDOWS - gp_windows(i)) * OFFS * PACK],
                 lhsT=ident_f[:],
-                rhs=gauss_tiles[i // SQ_CHUNKS][:, 0, chunk_windows(i, GP_WINDOWS, WINDOWS)].rearrange("k w p t -> k (w p t)"),
+                rhs=gauss_tiles[i // SQ_CHUNKS][:, 0, chunk_windows(i, gp_windows(i), WINDOWS)].rearrange("k w p t -> k (w p t)"),
                 start=True,
                 stop=True,
             )
             lon_tiles[i] = lon
 
         def products(i):
-            count = WINDOWS - GP_WINDOWS
+            count = WINDOWS - gp_windows(i)
             nc.vector.tensor_tensor(
-                out=product_tiles[i][:, GP_WINDOWS:].rearrange("k w (p q) t -> k w p q t", p=OFFS),
+                out=product_tiles[i][:, gp_windows(i) :].rearrange("k w (p q) t -> k w p q t", p=OFFS),
                 in0=lon_tiles.pop(i)[:, : count * OFFS * PACK]
                 .rearrange("k (w p t) -> k w p t", p=OFFS, t=PACK)
                 .unsqueeze(3)
                 .to_broadcast([P, count, OFFS, OFFS, PACK]),
-                in1=gauss_tiles[i // SQ_CHUNKS][:, 1, chunk_windows(i, GP_WINDOWS, WINDOWS)]
+                in1=gauss_tiles[i // SQ_CHUNKS][:, 1, chunk_windows(i, gp_windows(i), WINDOWS)]
                 .unsqueeze(2)
                 .to_broadcast([P, count, OFFS, OFFS, PACK]),
                 op=ALU.mult,
@@ -241,10 +264,10 @@ def tile_normal_nolayer_kernel(tc, x, coords_lon, coords_lat, mus_lon, mus_lat, 
         def sums_of_gpsimd(i):
             sums = psum.tile([P, PAIRS, P], F32, tag="sums")
             sum_tiles[i] = sums
-            sum_over_neighbours(i, 0, GP_WINDOWS // BATCH)
+            sum_over_neighbours(i, 0, gp_windows(i) // BATCH)
 
         def sums_of_vector(i):
-            sum_over_neighbours(i, GP_WINDOWS // BATCH, PAIRS)
+            sum_over_neighbours(i, gp_windows(i) // BATCH, PAIRS)
 
         def totals(i):
             total = work.tile([P, PAIRS], F32)
@@ -328,18 +351,41 @@ def tile_normal_nolayer_kernel(tc, x, coords_lon, coords_lat, mus_lon, mus_lat, 
             send(part[:], i * PAIRS + first, last - first)
 
         with tc.manual_schedule():
-            for step in range(-3 - SQ_CHUNKS, CHUNKS + 1):
-                ask = step + 1 + AHEAD * BLOCK
-                if 0 <= ask < CHUNKS and ask % BLOCK == 0:
-                    load_x(ask // BLOCK)
-                if 0 <= step + 3 + SQ_CHUNKS < CHUNKS:
-                    squares((step + 3 + SQ_CHUNKS) // SQ_CHUNKS, (step + 3 + SQ_CHUNKS) % SQ_CHUNKS)
+            row_tiles = load_coordinates()
+            for block in range(AHEAD + 1):
+                load_x(block)
+            turn_coordinates(row_tiles)
+            open_group(0)
+            squares(0, 0, 1, range(2 * OFFS))
+            gaussians(0)
+            lon_to_psum(0)
+            products_on_gpsimd(0)
+            sums_of_gpsimd(0)
+            products(0)
+            sums_of_vector(0)
+            squares(0, 1, SQ_CHUNKS, range(2 * OFFS))
+            gaussians(1)
+            products_on_gpsimd(1)
+            regroup_x(0)
+            regroup_x(1)
+            quarter_of_squares(SQ_CHUNKS)
+            gaussians(2)
+            products_on_gpsimd(2)
+            quarter_of_squares(SQ_CHUNKS + 1)
+            gaussians(3)
+            quarter_of_squares(SQ_CHUNKS + 2)
+            for step in range(1, CHUNKS + 1):
+                if step + 2 + SQ_CHUNKS < CHUNKS:
+                    quarter_of_squares(step + 2 + SQ_CHUNKS)
                 if 0 <= step - 2 < CHUNKS:
                     weights(step - 2)
                 if 0 <= step + 1 < CHUNKS:
                     regroup_x(step + 1)
                 if 0 <= step + 3 < CHUNKS:
                     gaussians(step + 3)
+                ask = step + 1 + AHEAD * BLOCK
+                if ask < CHUNKS and ask % BLOCK == 0:
+                    load_x(ask // BLOCK)
                 if 0 <= step < CHUNKS:
                     lon_to_psum(step)
                     sums_of_gpsimd(step)

@@ -236,12 +236,12 @@ def tile_normal_nolayer_kernel(tc, x, coords_lon, coords_lat, mus_lon, mus_lat, 
             count = WINDOWS - gp_windows(i)
             nc.vector.tensor_tensor(
                 out=product_tiles[i][:, gp_windows(i) :].rearrange("k w (p q) t -> k w p q t", p=OFFS),
-                in0=lon_tiles.pop(i)[:, : count * OFFS * PACK]
+                in0=gauss_tiles[i // SQ_CHUNKS][:, 1, chunk_windows(i, gp_windows(i), WINDOWS)]
+                .unsqueeze(2)
+                .to_broadcast([P, count, OFFS, OFFS, PACK]),
+                in1=lon_tiles.pop(i)[:, : count * OFFS * PACK]
                 .rearrange("k (w p t) -> k w p t", p=OFFS, t=PACK)
                 .unsqueeze(3)
-                .to_broadcast([P, count, OFFS, OFFS, PACK]),
-                in1=gauss_tiles[i // SQ_CHUNKS][:, 1, chunk_windows(i, gp_windows(i), WINDOWS)]
-                .unsqueeze(2)
                 .to_broadcast([P, count, OFFS, OFFS, PACK]),
                 op=ALU.mult,
             )

@@ -27,12 +27,13 @@ AHEAD = 3
 W_SETS = 3
 RUN = 4
 WINDOWS = PAIRS * BATCH
-GP_WINDOWS = 5
+GP_WINDOWS = (5, 6)
 GP_WINDOWS_0 = 3
 SHARED = 5
 HEAD_CHUNKS = 2
 BANK = 512
-SQ_CHUNKS = 4
+V_COPY_EVERY = 6
+SQ_CHUNKS = 8
 
 FLOPS = 2 * BATCH * NWIN * P * PACK * COLS_X * COLS_W
 
@@ -125,7 +126,7 @@ def tile_normal_nolayer_kernel(tc, x, coords_lon, coords_lat, mus_lon, mus_lat, 
         gauss_tiles = {}
 
         def open_group(group):
-            new_tile = work.tile([P, 2, SQ_CHUNKS * WINDOWS, OFFS, PACK], F32, name="gauss", bufs=3)
+            new_tile = work.tile([P, 2, SQ_CHUNKS * WINDOWS, OFFS, PACK], F32, name="gauss", bufs=2)
             gauss_tiles[group] = new_tile
 
         def squares(group, first, last, numbers):
@@ -141,12 +142,9 @@ def tile_normal_nolayer_kernel(tc, x, coords_lon, coords_lat, mus_lon, mus_lat, 
                     bias=neg_mu[a][:, o : o + 1],
                 )
 
-        def quarter_of_squares(quarter):
-            group, part = divmod(quarter, SQ_CHUNKS)
-            if part == 0:
-                open_group(group)
-            share = 2 * OFFS // SQ_CHUNKS
-            squares(group, 0, SQ_CHUNKS, range(part * share, (part + 1) * share))
+        def quarter(part):
+            share = 2 * OFFS // 4
+            return range(part * share, (part + 1) * share)
 
         def chunk_windows(i, first, last):
             start = (i % SQ_CHUNKS) * WINDOWS
@@ -170,28 +168,20 @@ def tile_normal_nolayer_kernel(tc, x, coords_lon, coords_lat, mus_lon, mus_lat, 
         result_tiles = {}
 
         def load_x(block):
-            raw = xin.tile([P, BATCH, BLOCK * PAIRS, PACK * COLS_X], BF16)
-            pairs = slice(block * BLOCK * PAIRS, (block + 1) * BLOCK * PAIRS)
-            queue = nc.sync if block <= AHEAD else nc.scalar
-            for b in range(BATCH):
-                queue.dma_start(out=raw[:, b], in_=x_view[b, :, pairs, :])
+            raw = xin.tile([P, BLOCK, BATCH, PAIRS, PACK * COLS_X], BF16)
+            for c in range(BLOCK):
+                first = (block * BLOCK + c) * PAIRS
+                for b in range(BATCH):
+                    nc.sync.dma_start(out=raw[:, c, b], in_=x_view[b, :, first : first + PAIRS, :])
             raw_tiles[block] = raw
 
         def regroup_x(i):
             grouped = work.tile([P, BATCH, PAIRS, COLS_X, PACK], BF16, align_bytes=64, bufs=4)
-            first = (i % BLOCK) * PAIRS
-            raw = raw_tiles[i // BLOCK]
-            for b in range(BATCH):
-                if i < HEAD_CHUNKS:
-                    nc.vector.tensor_copy(
-                        out=grouped[:, b],
-                        in_=raw[:, b, first : first + PAIRS, :].rearrange("k j (t c) -> k j c t", t=PACK),
-                    )
-                    continue
-                nc.scalar.copy(
-                    out=grouped[:, b].rearrange("k j (c r) t -> k j c t r", r=RUN),
-                    in_=raw[:, b, first : first + PAIRS, :].rearrange("k j (t c r) -> k j c t r", t=PACK, r=RUN),
-                )
+            copy = nc.vector.tensor_copy if i < HEAD_CHUNKS else nc.scalar.copy
+            copy(
+                out=grouped[:].rearrange("k b j (c r) t -> k (b j) c t r", r=RUN),
+                in_=raw_tiles[i // BLOCK][:, i % BLOCK].rearrange("k b j (t c r) -> k (b j) c t r", t=PACK, r=RUN),
+            )
             grouped_tiles[i] = grouped
 
         def quantise_x(i):
@@ -206,7 +196,7 @@ def tile_normal_nolayer_kernel(tc, x, coords_lon, coords_lat, mus_lon, mus_lat, 
             x_scale_tiles[i] = x_scales
 
         def gp_windows(i):
-            return GP_WINDOWS_0 if i == 0 else GP_WINDOWS
+            return GP_WINDOWS_0 if i == 0 else GP_WINDOWS[i % 2]
 
         def products_on_gpsimd(i):
             g = shared[(i - 2) % SHARED][:].rearrange("k (w m t) -> k w m t", w=WINDOWS, t=PACK)
@@ -222,7 +212,7 @@ def tile_normal_nolayer_kernel(tc, x, coords_lon, coords_lat, mus_lon, mus_lat, 
             product_tiles[i] = g
 
         def lon_to_psum(i):
-            lon = psum.tile([P, BANK], F32, tag="lon")
+            lon = psum.tile([P, BANK], F32, tag="lon", bufs=1)
             nc.tensor.matmul(
                 out=lon[:, : (WINDOWS - gp_windows(i)) * OFFS * PACK],
                 lhsT=ident_f[:],
@@ -310,7 +300,7 @@ def tile_normal_nolayer_kernel(tc, x, coords_lon, coords_lat, mus_lon, mus_lat, 
             scales = w_scales[i % W_SETS]
             x_codes = x_code_tiles[i]
             x_scales = x_scale_tiles[i]
-            acc = psum.tile([P, last - first, COLS_X], F32, tag="acc")
+            acc = psum.tile([P, last - first, COLS_X], F32, tag="acc", bufs=3)
             for j in range(first, last):
                 for b in range(BATCH):
                     half = slice(b * 2 * COLS_W, (b + 1) * 2 * COLS_W)
@@ -341,7 +331,8 @@ def tile_normal_nolayer_kernel(tc, x, coords_lon, coords_lat, mus_lon, mus_lat, 
                 result_tiles[block] = result
             result = result_tiles[block]
             slot = (i % BLOCK) * PAIRS
-            nc.scalar.copy(out=result[:, slot : slot + PAIRS], in_=acc_tiles.pop(i)[:])
+            copy = nc.vector.tensor_copy if i % V_COPY_EVERY == 1 else nc.scalar.copy
+            copy(out=result[:, slot : slot + PAIRS], in_=acc_tiles.pop(i)[:])
             if i % BLOCK == BLOCK - 1:
                 send(result[:], block * BLOCK * PAIRS, BLOCK * PAIRS)
 
@@ -363,24 +354,31 @@ def tile_normal_nolayer_kernel(tc, x, coords_lon, coords_lat, mus_lon, mus_lat, 
             sums_of_gpsimd(0)
             products(0)
             sums_of_vector(0)
-            squares(0, 1, SQ_CHUNKS, range(2 * OFFS))
+            squares(0, 1, SQ_CHUNKS // 2, range(2 * OFFS))
             gaussians(1)
             products_on_gpsimd(1)
             regroup_x(0)
             regroup_x(1)
-            quarter_of_squares(SQ_CHUNKS)
+            squares(0, SQ_CHUNKS // 2, SQ_CHUNKS, quarter(0))
             gaussians(2)
             products_on_gpsimd(2)
-            quarter_of_squares(SQ_CHUNKS + 1)
+            squares(0, SQ_CHUNKS // 2, SQ_CHUNKS, quarter(1))
             gaussians(3)
-            quarter_of_squares(SQ_CHUNKS + 2)
+            squares(0, SQ_CHUNKS // 2, SQ_CHUNKS, quarter(2))
             for step in range(1, CHUNKS + 1):
-                if step + 2 + SQ_CHUNKS < CHUNKS:
-                    quarter_of_squares(step + 2 + SQ_CHUNKS)
+                if step == 1:
+                    squares(0, SQ_CHUNKS // 2, SQ_CHUNKS, quarter(3))
+                group, part = divmod(step + 6, SQ_CHUNKS)
+                if group * SQ_CHUNKS < CHUNKS and part < 4:
+                    if part == 0:
+                        open_group(group)
+                    squares(group, 0, SQ_CHUNKS, quarter(part))
                 if 0 <= step - 2 < CHUNKS:
                     weights(step - 2)
                 if 0 <= step + 1 < CHUNKS:
                     regroup_x(step + 1)
+                if 0 <= step - 4 < CHUNKS:
+                    store(step - 4)
                 if 0 <= step + 3 < CHUNKS:
                     gaussians(step + 3)
                 ask = step + 1 + AHEAD * BLOCK
@@ -404,11 +402,10 @@ def tile_normal_nolayer_kernel(tc, x, coords_lon, coords_lat, mus_lon, mus_lat, 
                     contract(step - 2, 0, PAIRS)
                 if 0 <= step + 2 < CHUNKS:
                     products_on_gpsimd(step + 2)
-                if 0 <= step - 3 < CHUNKS:
-                    store(step - 3)
+            store(CHUNKS - 3)
             store_at_once(CHUNKS - 2, 0, PAIRS)
             weights(CHUNKS - 1)
-            for first in (PAIRS // 2, 0):
-                quantise_w(CHUNKS - 1, first, first + PAIRS // 2)
-                contract(CHUNKS - 1, first, first + PAIRS // 2)
-                store_at_once(CHUNKS - 1, first, first + PAIRS // 2)
+            for first, last in ((0, PAIRS - 1), (PAIRS - 1, PAIRS)):
+                quantise_w(CHUNKS - 1, first, last)
+                contract(CHUNKS - 1, first, last)
+                store_at_once(CHUNKS - 1, first, last)

@@ -32,6 +32,8 @@ GP_WINDOWS_0 = 3
 SHARED = 5
 HEAD_CHUNKS = 2
 BANK = 512
+ACC_SETS = 3
+SQ_STEPS = 5
 V_COPY_EVERY = 6
 SQ_CHUNKS = 8
 
@@ -178,10 +180,11 @@ def tile_normal_nolayer_kernel(tc, x, coords_lon, coords_lat, mus_lon, mus_lat, 
         def regroup_x(i):
             grouped = work.tile([P, BATCH, PAIRS, COLS_X, PACK], BF16, align_bytes=64, bufs=4)
             copy = nc.vector.tensor_copy if i < HEAD_CHUNKS else nc.scalar.copy
-            copy(
-                out=grouped[:].rearrange("k b j (c r) t -> k (b j) c t r", r=RUN),
-                in_=raw_tiles[i // BLOCK][:, i % BLOCK].rearrange("k b j (t c r) -> k (b j) c t r", t=PACK, r=RUN),
-            )
+            for b in (slice(0, 1), slice(1, BATCH)) if i == 0 else (slice(0, BATCH),):
+                copy(
+                    out=grouped[:, b].rearrange("k b j (c r) t -> k (b j) c t r", r=RUN),
+                    in_=raw_tiles[i // BLOCK][:, i % BLOCK, b].rearrange("k b j (t c r) -> k (b j) c t r", t=PACK, r=RUN),
+                )
             grouped_tiles[i] = grouped
 
         def quantise_x(i):
@@ -300,7 +303,7 @@ def tile_normal_nolayer_kernel(tc, x, coords_lon, coords_lat, mus_lon, mus_lat, 
             scales = w_scales[i % W_SETS]
             x_codes = x_code_tiles[i]
             x_scales = x_scale_tiles[i]
-            acc = psum.tile([P, last - first, COLS_X], F32, tag="acc", bufs=3)
+            acc = psum.tile([P, last - first, COLS_X], F32, tag="acc%d" % ((i + (first > 0)) % ACC_SETS), bufs=1)
             for j in range(first, last):
                 for b in range(BATCH):
                     half = slice(b * 2 * COLS_W, (b + 1) * 2 * COLS_W)
@@ -331,7 +334,8 @@ def tile_normal_nolayer_kernel(tc, x, coords_lon, coords_lat, mus_lon, mus_lat, 
                 result_tiles[block] = result
             result = result_tiles[block]
             slot = (i % BLOCK) * PAIRS
-            copy = nc.vector.tensor_copy if i % V_COPY_EVERY == 1 else nc.scalar.copy
+            on_vector = i % V_COPY_EVERY == 1 and i < CHUNKS - V_COPY_EVERY
+            copy = nc.vector.tensor_copy if on_vector else nc.scalar.copy
             copy(out=result[:, slot : slot + PAIRS], in_=acc_tiles.pop(i)[:])
             if i % BLOCK == BLOCK - 1:
                 send(result[:], block * BLOCK * PAIRS, BLOCK * PAIRS)
@@ -352,12 +356,13 @@ def tile_normal_nolayer_kernel(tc, x, coords_lon, coords_lat, mus_lon, mus_lat, 
             lon_to_psum(0)
             products_on_gpsimd(0)
             sums_of_gpsimd(0)
+            regroup_x(0)
             products(0)
             sums_of_vector(0)
             squares(0, 1, SQ_CHUNKS // 2, range(2 * OFFS))
             gaussians(1)
             products_on_gpsimd(1)
-            regroup_x(0)
+            lon_to_psum(1)
             regroup_x(1)
             squares(0, SQ_CHUNKS // 2, SQ_CHUNKS, quarter(0))
             gaussians(2)
@@ -366,26 +371,25 @@ def tile_normal_nolayer_kernel(tc, x, coords_lon, coords_lat, mus_lon, mus_lat, 
             gaussians(3)
             squares(0, SQ_CHUNKS // 2, SQ_CHUNKS, quarter(2))
             for step in range(1, CHUNKS + 1):
-                if step == 1:
-                    squares(0, SQ_CHUNKS // 2, SQ_CHUNKS, quarter(3))
-                group, part = divmod(step + 6, SQ_CHUNKS)
-                if group * SQ_CHUNKS < CHUNKS and part < 4:
-                    if part == 0:
-                        open_group(group)
-                    squares(group, 0, SQ_CHUNKS, quarter(part))
-                if 0 <= step - 2 < CHUNKS:
-                    weights(step - 2)
-                if 0 <= step + 1 < CHUNKS:
-                    regroup_x(step + 1)
                 if 0 <= step - 4 < CHUNKS:
                     store(step - 4)
+                if step == 1:
+                    squares(0, SQ_CHUNKS // 2, SQ_CHUNKS, quarter(3))
+                group, part = divmod(step + SQ_STEPS + 2, SQ_CHUNKS)
+                if group * SQ_CHUNKS < CHUNKS and part < SQ_STEPS:
+                    if part == 0:
+                        open_group(group)
+                    squares(group, 0, SQ_CHUNKS, range(2 * OFFS)[part::SQ_STEPS])
+                if 0 <= step - 2 < CHUNKS:
+                    weights(step - 2)
                 if 0 <= step + 3 < CHUNKS:
                     gaussians(step + 3)
+                if 0 <= step + 1 < CHUNKS:
+                    regroup_x(step + 1)
                 ask = step + 1 + AHEAD * BLOCK
                 if ask < CHUNKS and ask % BLOCK == 0:
                     load_x(ask // BLOCK)
                 if 0 <= step < CHUNKS:
-                    lon_to_psum(step)
                     sums_of_gpsimd(step)
                 if 0 <= step - 1 < CHUNKS:
                     totals(step - 1)
@@ -395,6 +399,8 @@ def tile_normal_nolayer_kernel(tc, x, coords_lon, coords_lat, mus_lon, mus_lat, 
                     normalisers(step - 1)
                 if 0 <= step < CHUNKS:
                     sums_of_vector(step)
+                if 0 <= step + 1 < CHUNKS:
+                    lon_to_psum(step + 1)
                 if 0 <= step - 1 < CHUNKS:
                     quantise_x(step - 1)
                 if 0 <= step - 2 < CHUNKS:

import concourse.mybir as mybir
from concourse.masks import make_identity

F32 = mybir.dt.float32
BF16 = mybir.dt.bfloat16
U32 = mybir.dt.uint32
U8 = mybir.dt.uint8
I32 = mybir.dt.int32
FP8X4 = mybir.dt.float8_e4m3fn_x4
ACT = mybir.ActivationFunctionType
ALU = mybir.AluOpType

P = 128
PACK = 4
BATCH = 2
NWIN = 96
OFFS = 8
COLS_W = OFFS * OFFS
COLS_X = 128
CHAN = 32
MIN_SIGMA = 1e-10

PAIRS = 4
CHUNKS = NWIN // PAIRS
BLOCK = 2
AHEAD = 3
W_SETS = 3
RUN = 4
WINDOWS = PAIRS * BATCH
GP_WINDOWS = (5, 6)
GP_WINDOWS_0 = 3
SHARED = 5
HEAD_CHUNKS = 2
BANK = 512
ACC_SETS = 3
SQ_STEPS = 5
V_COPY_EVERY = 6
SQ_CHUNKS = 8

FLOPS = 2 * BATCH * NWIN * P * PACK * COLS_X * COLS_W


def tile_normal_nolayer_kernel(tc, x, coords_lon, coords_lat, mus_lon, mus_lat, sigma, out):
    nc = tc.nc

    x_view = x.rearrange("b n o (k t) v c -> b k (n o) (t v c)", t=PACK)
    out_view = out.rearrange("b n v p q c -> b (p q) (n v) c")
    coord_rows = [
        coords_lon.rearrange("b n o i h -> (b n o) (i h)"),
        coords_lat.rearrange("b n o i h -> (b n o) (i h)"),
    ]

    with tc.tile_pool(name="keep", bufs=1) as keep, tc.tile_pool(name="head", bufs=1) as head, tc.tile_pool(
        name="xin", bufs=AHEAD + 1
    ) as xin, tc.tile_pool(name="work", bufs=3) as work, tc.psum_pool(name="psum", bufs=2) as psum:
        ident_bf = keep.tile([P, P], BF16)
        make_identity(nc, ident_bf[:])
        ident_f = keep.tile([P, P], F32)
        make_identity(nc, ident_f[:])

        sig_bf = keep.tile([P, 1], BF16)
        nc.scalar.dma_start(out=sig_bf[:], in_=sigma.partition_broadcast(P))
        mu_lon = keep.tile([P, OFFS], BF16)
        nc.scalar.dma_start(out=mu_lon[:], in_=mus_lon.partition_broadcast(P))
        mu_lat = keep.tile([P, OFFS], BF16)
        nc.scalar.dma_start(out=mu_lat[:], in_=mus_lat.partition_broadcast(P))
        mu_tiles = [mu_lon, mu_lat]

        warm = keep.tile([P, 1], F32)
        nc.vector.memset(warm[:], 0.0)
        nc.scalar.activation(out=warm[:], in_=warm[:], func=ACT.Exp)

        sig_f = keep.tile([P, 1], F32)
        nc.vector.tensor_scalar_max(out=sig_f[:], in0=sig_bf[:], scalar1=MIN_SIGMA)
        inv_sig = keep.tile([P, 1], F32)
        nc.vector.reciprocal(out=inv_sig[:], in_=sig_f[:])
        neg_mu = []
        for a in range(2):
            shifted = keep.tile([P, OFFS], F32, name="neg_mu%d" % a)
            nc.vector.tensor_scalar(
                out=shifted[:], in0=mu_tiles[a][:], scalar1=inv_sig[:], scalar2=-1.0, op0=ALU.mult, op1=ALU.mult
            )
            neg_mu.append(shifted)

        def outer_columns(words):
            return words.rearrange("k j (e m) -> k j e m", e=4)[:, :, 0:4:3]

        w_codes = []
        w_scales = []
        for i in range(W_SETS):
            codes = keep.tile([P, PAIRS, 4 * COLS_W], U32, name="w_codes%d" % i, align_bytes=64)
            nc.vector.memset(outer_columns(codes[:].bitcast(I32)), 0)
            w_codes.append(codes)
            scales = keep.tile([P, PAIRS, 4 * COLS_W], U8, name="w_scales%d" % i, align_bytes=64)
            nc.vector.memset(outer_columns(scales[:].bitcast(I32)), 0)
            w_scales.append(scales)

        shared = []
        for i in range(SHARED):
            shared_tile = keep.tile([P, WINDOWS * COLS_W * PACK], F32, name="shared%d" % i, align_bytes=64)
            shared.append(shared_tile)

        coord = keep.tile([P, 2, NWIN, BATCH, PACK], BF16)

        def load_coordinates():
            row_tiles = []
            for a in range(2):
                for b in range(BATCH):
                    first_row = b * (BATCH * NWIN - P)
                    rows = head.tile([P, P * PACK], BF16, name="rows%d%d" % (a, b))
                    nc.sync.dma_start(out=rows[:], in_=coord_rows[a][first_row : first_row + P, :])
                    row_tiles.append(rows)
            return row_tiles

        def turn_coordinates(row_tiles):
            for a in range(2):
                for b in range(BATCH):
                    by_t = row_tiles[a * BATCH + b][:].rearrange("w (i t) -> w t i", t=PACK)
                    turned = psum.tile([P, PACK, P], BF16, tag=("spread", "sums")[a])
                    for t in range(PACK):
                        nc.tensor.transpose(turned[:, t, :], by_t[:, t, :], ident_bf[:])
                    first_col = b * (P - NWIN)
                    nc.vector.tensor_copy(
                        out=coord[:, a, :, b, :],
                        in_=turned[:, :, first_col : first_col + NWIN].rearrange("k t n -> k n t"),
                    )

        gauss_tiles = {}

        def open_group(group):
            new_tile = work.tile([P, 2, SQ_CHUNKS * WINDOWS, OFFS, PACK], F32, name="gauss", bufs=2)
            gauss_tiles[group] = new_tile

        def squares(group, first, last, numbers):
            start = group * SQ_CHUNKS
            pairs = slice((start + first) * PAIRS, (start + last) * PAIRS)
            for number in numbers:
                a, o = divmod(number, OFFS)
                nc.scalar.activation(
                    out=gauss_tiles[group][:, a, first * WINDOWS : last * WINDOWS, o, :],
                    in_=coord[:, a, pairs].rearrange("k n b t -> k (n b) t"),
                    func=ACT.Square,
                    scale=inv_sig[:],
                    bias=neg_mu[a][:, o : o + 1],
                )

        def quarter(part):
            share = 2 * OFFS // 4
            return range(part * share, (part + 1) * share)

        def chunk_windows(i, first, last):
            start = (i % SQ_CHUNKS) * WINDOWS
            return slice(start + first, start + last)

        def gaussians(i):
            part = gauss_tiles[i // SQ_CHUNKS][:, :, chunk_windows(i, 0, WINDOWS)]
            nc.scalar.activation(out=part, in_=part, func=ACT.Exp, scale=-0.5)

        raw_tiles = {}
        grouped_tiles = {}
        x_code_tiles = {}
        x_scale_tiles = {}
        product_tiles = {}
        lon_tiles = {}
        sum_tiles = {}
        spread_tiles = {}
        acc_tiles = {}
        total_tiles = {}
        w_tiles = {}
        result_tiles = {}

        def load_x(block):
            raw = xin.tile([P, BLOCK, BATCH, PAIRS, PACK * COLS_X], BF16)
            for c in range(BLOCK):
                first = (block * BLOCK + c) * PAIRS
                for b in range(BATCH):
                    nc.sync.dma_start(out=raw[:, c, b], in_=x_view[b, :, first : first + PAIRS, :])
            raw_tiles[block] = raw

        def regroup_x(i):
            grouped = work.tile([P, BATCH, PAIRS, COLS_X, PACK], BF16, align_bytes=64, bufs=4)
            copy = nc.vector.tensor_copy if i < HEAD_CHUNKS else nc.scalar.copy
            for b in (slice(0, 1), slice(1, BATCH)) if i == 0 else (slice(0, BATCH),):
                copy(
                    out=grouped[:, b].rearrange("k b j (c r) t -> k (b j) c t r", r=RUN),
                    in_=raw_tiles[i // BLOCK][:, i % BLOCK, b].rearrange("k b j (t c r) -> k (b j) c t r", t=PACK, r=RUN),
                )
            grouped_tiles[i] = grouped

        def quantise_x(i):
            x_codes = work.tile([P, BATCH, PAIRS, COLS_X], U32, align_bytes=64)
            x_scales = work.tile([P, BATCH, PAIRS, COLS_X], U8, align_bytes=64)
            nc.vector.quantize_mx(
                out=x_codes[:].rearrange("k b j c -> k (b j c)").bitcast(FP8X4),
                scales=x_scales[:].rearrange("k b j c -> k (b j c)"),
                in_=grouped_tiles.pop(i)[:].rearrange("k b j c t -> k (b j c t)"),
            )
            x_code_tiles[i] = x_codes
            x_scale_tiles[i] = x_scales

        def gp_windows(i):
            return GP_WINDOWS_0 if i == 0 else GP_WINDOWS[i % 2]

        def products_on_gpsimd(i):
            g = shared[(i - 2) % SHARED][:].rearrange("k (w m t) -> k w m t", w=WINDOWS, t=PACK)
            gauss = gauss_tiles[i // SQ_CHUNKS]
            count = gp_windows(i)
            span = chunk_windows(i, 0, count)
            nc.gpsimd.tensor_tensor(
                out=g[:, :count].rearrange("k w (p q) t -> k w p q t", p=OFFS),
                in0=gauss[:, 0, span].unsqueeze(3).to_broadcast([P, count, OFFS, OFFS, PACK]),
                in1=gauss[:, 1, span].unsqueeze(2).to_broadcast([P, count, OFFS, OFFS, PACK]),
                op=ALU.mult,
            )
            product_tiles[i] = g

        def lon_to_psum(i):
            lon = psum.tile([P, BANK], F32, tag="lon", bufs=1)
            nc.tensor.matmul(
                out=lon[:, : (WINDOWS - gp_windows(i)) * OFFS * PACK],
                lhsT=ident_f[:],
                rhs=gauss_tiles[i // SQ_CHUNKS][:, 0, chunk_windows(i, gp_windows(i), WINDOWS)].rearrange("k w p t -> k (w p t)"),
                start=True,
                stop=True,
            )
            lon_tiles[i] = lon

        def products(i):
            count = WINDOWS - gp_windows(i)
            nc.vector.tensor_tensor(
                out=product_tiles[i][:, gp_windows(i) :].rearrange("k w (p q) t -> k w p q t", p=OFFS),
                in0=gauss_tiles[i // SQ_CHUNKS][:, 1, chunk_windows(i, gp_windows(i), WINDOWS)]
                .unsqueeze(2)
                .to_broadcast([P, count, OFFS, OFFS, PACK]),
                in1=lon_tiles.pop(i)[:, : count * OFFS * PACK]
                .rearrange("k (w p t) -> k w p t", p=OFFS, t=PACK)
                .unsqueeze(3)
                .to_broadcast([P, count, OFFS, OFFS, PACK]),
                op=ALU.mult,
            )
            if i % SQ_CHUNKS == SQ_CHUNKS - 1:
                gauss_tiles.pop(i // SQ_CHUNKS)

        def sum_over_neighbours(i, first, last):
            g = product_tiles[i].rearrange("k (j b) m t -> k j (b m) t", b=BATCH)
            for j in range(first, last):
                for t in range(PACK):
                    nc.tensor.matmul(
                        out=sum_tiles[i][:, j, :],
                        lhsT=g[:, j, :, t],
                        rhs=ident_f[:],
                        is_transpose=True,
                        start=(t == 0),
                        stop=(t == PACK - 1),
                    )

        def sums_of_gpsimd(i):
            sums = psum.tile([P, PAIRS, P], F32, tag="sums")
            sum_tiles[i] = sums
            sum_over_neighbours(i, 0, gp_windows(i) // BATCH)

        def sums_of_vector(i):
            sum_over_neighbours(i, gp_windows(i) // BATCH, PAIRS)

        def totals(i):
            total = work.tile([P, PAIRS], F32)
            nc.vector.tensor_reduce(out=total[:], in_=sum_tiles.pop(i)[:], axis=mybir.AxisListType.X, op=ALU.add)
            total_tiles[i] = total

        def normalisers(i):
            inverse = work.tile([P, PAIRS], F32)
            nc.vector.reciprocal(out=inverse[:], in_=total_tiles.pop(i)[:])
            spread = psum.tile([P, PAIRS, BATCH * COLS_W], F32, tag="spread")
            for j in range(PAIRS):
                nc.tensor.transpose(spread[:, j, :], inverse[:, j : j + 1].to_broadcast([P, P]), ident_f[:])
            spread_tiles[i] = spread

        def weights(i):
            width = WINDOWS * COLS_W
            w_bf = shared[(i + 2) % SHARED][:, : width * PACK // 2].bitcast(BF16)
            w_tiles[i] = w_bf.rearrange("k (j m t) -> k j m t", j=PAIRS, t=PACK)
            nc.vector.tensor_tensor(
                out=w_bf.rearrange("k (m t) -> k m t", t=PACK),
                in0=product_tiles.pop(i).rearrange("k w m t -> k (w m) t"),
                in1=spread_tiles.pop(i)[:].rearrange("k j m -> k (j m)").unsqueeze(2).to_broadcast([P, width, PACK]),
                op=ALU.mult,
            )

        def quantise_w(i, first, last):
            w_bf = w_tiles[i]
            codes = w_codes[i % W_SETS]
            scales = w_scales[i % W_SETS]
            inner = slice(COLS_W, 3 * COLS_W)
            for j in range(first, last):
                nc.vector.quantize_mx(
                    out=codes[:, j, inner].bitcast(FP8X4),
                    scales=scales[:, j, inner],
                    in_=w_bf[:, j].rearrange("k m t -> k (m t)"),
                )

        def contract(i, first, last):
            codes = w_codes[i % W_SETS]
            scales = w_scales[i % W_SETS]
            x_codes = x_code_tiles[i]
            x_scales = x_scale_tiles[i]
            acc = psum.tile([P, last - first, COLS_X], F32, tag="acc%d" % ((i + (first > 0)) % ACC_SETS), bufs=1)
            for j in range(first, last):
                for b in range(BATCH):
                    half = slice(b * 2 * COLS_W, (b + 1) * 2 * COLS_W)
                    nc.tensor.matmul_mx(
                        out=acc[:, j - first, :],
                        lhsT=codes[:, j, half].bitcast(FP8X4),
                        lhsT_scale=scales[:, j, half],
                        rhs=x_codes[:, b, j, :].bitcast(FP8X4),
                        rhs_scale=x_scales[:, b, j, :],
                        start=(b == 0),
                        stop=(b == BATCH - 1),
                    )
            acc_tiles[i] = acc

        def send(result, first_pair, count):
            per_pair = COLS_X // CHAN
            for b in range(BATCH):
                lanes = slice((1 - b) * COLS_W, (2 - b) * COLS_W)
                nc.sync.dma_start(
                    out=out_view[b, :, first_pair * per_pair : (first_pair + count) * per_pair, :],
                    in_=result[lanes].rearrange("m j (v c) -> m (j v) c", c=CHAN),
                )

        def store(i):
            block = i // BLOCK
            if i % BLOCK == 0:
                result = work.tile([P, BLOCK * PAIRS, COLS_X], F32)
                result_tiles[block] = result
            result = result_tiles[block]
            slot = (i % BLOCK) * PAIRS
            on_vector = i % V_COPY_EVERY == 1 and i < CHUNKS - V_COPY_EVERY
            copy = nc.vector.tensor_copy if on_vector else nc.scalar.copy
            copy(out=result[:, slot : slot + PAIRS], in_=acc_tiles.pop(i)[:])
            if i % BLOCK == BLOCK - 1:
                send(result[:], block * BLOCK * PAIRS, BLOCK * PAIRS)

        def store_at_once(i, first, last):
            part = work.tile([P, last - first, COLS_X], F32, name="part", bufs=3)
            nc.scalar.copy(out=part[:], in_=acc_tiles.pop(i)[:])
            send(part[:], i * PAIRS + first, last - first)

        with tc.manual_schedule():
            row_tiles = load_coordinates()
            for block in range(AHEAD + 1):
                load_x(block)
            turn_coordinates(row_tiles)
            open_group(0)
            squares(0, 0, 1, range(2 * OFFS))
            gaussians(0)
            lon_to_psum(0)
            products_on_gpsimd(0)
            sums_of_gpsimd(0)
            regroup_x(0)
            products(0)
            sums_of_vector(0)
            squares(0, 1, SQ_CHUNKS // 2, range(2 * OFFS))
            gaussians(1)
            products_on_gpsimd(1)
            lon_to_psum(1)
            regroup_x(1)
            squares(0, SQ_CHUNKS // 2, SQ_CHUNKS, quarter(0))
            gaussians(2)
            products_on_gpsimd(2)
            squares(0, SQ_CHUNKS // 2, SQ_CHUNKS, quarter(1))
            gaussians(3)
            squares(0, SQ_CHUNKS // 2, SQ_CHUNKS, quarter(2))
            for step in range(1, CHUNKS + 1):
                if 0 <= step - 4 < CHUNKS:
                    store(step - 4)
                if step == 1:
                    squares(0, SQ_CHUNKS // 2, SQ_CHUNKS, quarter(3))
                group, part = divmod(step + SQ_STEPS + 2, SQ_CHUNKS)
                if group * SQ_CHUNKS < CHUNKS and part < SQ_STEPS:
                    if part == 0:
                        open_group(group)
                    squares(group, 0, SQ_CHUNKS, range(2 * OFFS)[part::SQ_STEPS])
                if 0 <= step - 2 < CHUNKS:
                    weights(step - 2)
                if 0 <= step + 3 < CHUNKS:
                    gaussians(step + 3)
                if 0 <= step + 1 < CHUNKS:
                    regroup_x(step + 1)
                ask = step + 1 + AHEAD * BLOCK
                if ask < CHUNKS and ask % BLOCK == 0:
                    load_x(ask // BLOCK)
                if 0 <= step < CHUNKS:
                    sums_of_gpsimd(step)
                if 0 <= step - 1 < CHUNKS:
                    totals(step - 1)
                if 0 <= step < CHUNKS:
                    products(step)
                if 0 <= step - 1 < CHUNKS:
                    normalisers(step - 1)
                if 0 <= step < CHUNKS:
                    sums_of_vector(step)
                if 0 <= step + 1 < CHUNKS:
                    lon_to_psum(step + 1)
                if 0 <= step - 1 < CHUNKS:
                    quantise_x(step - 1)
                if 0 <= step - 2 < CHUNKS:
                    quantise_w(step - 2, 0, PAIRS)
                    contract(step - 2, 0, PAIRS)
                if 0 <= step + 2 < CHUNKS:
                    products_on_gpsimd(step + 2)
            store(CHUNKS - 3)
            store_at_once(CHUNKS - 2, 0, PAIRS)
            weights(CHUNKS - 1)
            for first, last in ((0, PAIRS - 1), (PAIRS - 1, PAIRS)):
                quantise_w(CHUNKS - 1, first, last)
                contract(CHUNKS - 1, first, last)
                store_at_once(CHUNKS - 1, first, last)
